import numpy as np
import ml_dtypes


def mxq(x, axis, fmt="e4m3"):
    dtype, down = {"e4m3": (ml_dtypes.float8_e4m3fn, 7), "e5m2": (ml_dtypes.float8_e5m2, 14)}[fmt]
    v = np.moveaxis(np.asarray(x, np.float32).astype(ml_dtypes.bfloat16).astype(np.float64), axis, -1)
    blocks = v.reshape(v.shape[:-1] + (-1, 32))
    amax = np.abs(blocks).max(-1, keepdims=True)
    byte = np.maximum(np.where(amax > 0, np.frexp(amax)[1] - 1 + 127, 0) - down, 1)
    scale = np.exp2(byte - 127.0)
    codes = (blocks / scale).astype(np.float32).astype(dtype).astype(np.float64)
    return np.moveaxis((codes * scale).reshape(v.shape), -1, axis)


WIDE = False


def mx_kscale(k):
    if not WIDE:
        return np.ones(k)
    levels = np.array([10, -10, 5, -5, 0])
    a = np.random.permutation(np.resize(levels, k // 512 * 4)).reshape(k // 512, 4)
    idx = np.arange(k)
    return np.exp2(a[idx // 512, idx % 128 // 32])


BF16 = ml_dtypes.bfloat16


def bf(x):
    return np.asarray(x, np.float32).astype(BF16)


def f64(x):
    return np.asarray(x).astype(np.float64)


B, N, IN_DIM, OUT_DIM, NUM_F = 16, 256, 1024, 512, 1


def silu(v):
    return v / (1.0 + np.exp(-v))


def setup_inputs():
    t = mx_kscale(IN_DIM)
    return {"x": bf(np.random.standard_normal((B, N, IN_DIM))),
            "base_weight": bf(np.random.standard_normal((OUT_DIM, IN_DIM)) / np.sqrt(IN_DIM)),
            "grid": bf(np.arange(NUM_F) + 1.5),
            "scale_sp": bf(1.0 + 0.1 * np.random.standard_normal(OUT_DIM)),
            "coef": bf(np.random.uniform(size=(IN_DIM, NUM_F)) * t[:, None]),
            "conv_w": bf(np.random.standard_normal((NUM_F, OUT_DIM, IN_DIM)) / np.sqrt(IN_DIM) / t[None, None, :]),
            "conv_b": bf(np.random.standard_normal((NUM_F, OUT_DIM)) * 0.1)}


def reference(x, base_weight, grid, scale_sp, coef, conv_w, conv_b):
    x = f64(x)
    b, n, d = x.shape
    xf = x.reshape(b * n, d)
    base_out = mxq(silu(xf), 1, "e4m3") @ mxq(f64(base_weight), 1, "e4m3").T
    s = np.sin(xf[:, None, :] * f64(grid)[None, :, None]) * f64(coef).T[None, :, :]
    sq = mxq(s, 2, "e4m3")
    wq = mxq(f64(conv_w), 2, "e4m3")
    spline = np.matmul(sq.transpose(1, 0, 2), wq.transpose(0, 2, 1)).transpose(1, 0, 2) + f64(conv_b)[None, :, :]
    out = base_out + spline.sum(axis=1) * f64(scale_sp)
    return out.reshape(b, n, OUT_DIM)

@@ -1,0 +1,341 @@
+import math
+from contextlib import ExitStack
+
+import concourse.masks as masks
+import concourse.mybir as mybir
+
+FLOPS = 2 * 2 * 4096 * 1024 * 512
+
+P = 128
+F32 = mybir.dt.float32
+BF16 = mybir.dt.bfloat16
+I32 = mybir.dt.int32
+U32 = mybir.dt.uint32
+U8 = mybir.dt.uint8
+FP8X4 = mybir.dt.float8_e4m3fn_x4
+ALU = mybir.AluOpType
+ACT = mybir.ActivationFunctionType
+
+TILES = 32
+GROUP = 4
+CHUNKS = 4
+KDIM = 1024
+NOUT = 512
+TWO_PI = 2.0 * math.pi
+
+
+def tile_efficient_skan_batch_t_kernel(tc, x, base_weight, grid, scale_sp, coef, conv_w, conv_b, out):
+    nc = tc.nc
+    xf = x.flatten_outer_dims()
+    of = out.flatten_outer_dims()
+    with ExitStack() as ctx:
+        const = ctx.enter_context(tc.tile_pool(name="const", bufs=1))
+        wstage = ctx.enter_context(tc.tile_pool(name="wstage", bufs=1))
+        xpool = ctx.enter_context(tc.tile_pool(name="xpool", bufs=4))
+        kpool = ctx.enter_context(tc.tile_pool(name="kpool", bufs=3))
+        fpool = ctx.enter_context(tc.tile_pool(name="fpool", bufs=4))
+        gpool = ctx.enter_context(tc.tile_pool(name="gpool", bufs=4))
+        qpool = ctx.enter_context(tc.tile_pool(name="qpool", bufs=2))
+        tbpool = ctx.enter_context(tc.tile_pool(name="tbpool", bufs=2))
+        otpool = ctx.enter_context(tc.tile_pool(name="otpool", bufs=8))
+        ospool = ctx.enter_context(tc.tile_pool(name="ospool", bufs=2))
+        ps_xt = ctx.enter_context(tc.psum_pool(name="ps_xt", bufs=2))
+        ps_sn = ctx.enter_context(tc.psum_pool(name="ps_sn", bufs=2))
+        ps_mb = ctx.enter_context(tc.psum_pool(name="ps_mb", bufs=1))
+        ps_ms = ctx.enter_context(tc.psum_pool(name="ps_ms", bufs=2))
+        ps_op = ctx.enter_context(tc.psum_pool(name="ps_op", bufs=1))
+        ctx.enter_context(tc.manual_schedule())
+
+        xt = {}
+        kt = {}
+        ft = {}
+        xps = {}
+        snps = {}
+        gat = {}
+        gst = {}
+        aq = {}
+        asc = {}
+        sq = {}
+        ssc = {}
+        bps = {}
+        sps = {}
+        tbt = {}
+        ott = {}
+        ops = {}
+        ost = {}
+
+        def load_x(grp):
+            t = xpool.tile([P, GROUP * KDIM], BF16, name="x_nat", tag="x_nat")
+            rows = xf[grp * 512 : (grp + 1) * 512, :]
+            if grp == 0:
+                for j in range(GROUP):
+                    nc.sync.dma_start(
+                        out=t[:, j * KDIM : (j + 1) * KDIM],
+                        in_=rows.rearrange("(p j) k -> p j k", j=GROUP)[:, j, :],
+                    )
+            else:
+                nc.sync.dma_start(out=t[:], in_=rows.rearrange("(p j) k -> p (j k)", j=GROUP))
+            xt[grp] = t
+
+        vecs = const.tile([P, P], BF16, name="vecs")
+        nc.vector.memset(vecs[:], 0.0)
+        g_bf = const.tile([P, 1], BF16, name="g_bf")
+        nc.sync.dma_start(out=g_bf[:], in_=grid.partition_broadcast(P))
+        nc.sync.dma_start(out=vecs[0:4, :], in_=scale_sp.rearrange("(a p) -> a p", p=P))
+        nc.sync.dma_start(out=vecs[4:8, :], in_=conv_b.rearrange("o (a p) -> (o a) p", p=P))
+        nc.sync.dma_start(out=vecs[8:16, :], in_=coef.rearrange("(a p) o -> a (p o)", p=P))
+        load_x(0)
+        wb_nat = wstage.tile([P, CHUNKS * KDIM], BF16, name="wb_nat")
+        nc.sync.dma_start(
+            out=wb_nat[:].rearrange("p (c k) -> p c k", c=CHUNKS),
+            in_=base_weight.rearrange("(c p) k -> p c k", p=P),
+        )
+        load_x(1)
+        wc_nat = wstage.tile([P, CHUNKS * KDIM], BF16, name="wc_nat")
+        nc.sync.dma_start(
+            out=wc_nat[:].rearrange("p (c k) -> p c k", c=CHUNKS),
+            in_=conv_w.rearrange("o (c p) k -> p (o c) k", p=P),
+        )
+        load_x(2)
+        load_x(3)
+
+        ident_f = const.tile([P, P], F32, name="ident_f")
+        masks.make_identity(nc, ident_f[:])
+        ident_b = const.tile([P, P], BF16, name="ident_b")
+        masks.make_identity(nc, ident_b[:])
+
+        cyc = const.tile([P, 1], F32, name="cyc")
+        nc.vector.tensor_scalar(out=cyc[:], in0=g_bf[:], scalar1=1.0 / TWO_PI, scalar2=None, op0=ALU.mult)
+
+        vps = ps_op.tile([P, P], BF16, name="vps", tag="op")
+        nc.tensor.transpose(vps[:], vecs[:], ident_b[:])
+        vt = const.tile([P, 16], F32, name="vt")
+        nc.vector.tensor_copy(out=vt[:], in_=vps[:, 0:16])
+        spb = const.tile([P, CHUNKS], F32, name="spb")
+        nc.vector.tensor_mul(out=spb[:], in0=vt[:, 0:4], in1=vt[:, 4:8])
+
+        gwb = wstage.tile([P, 4096], BF16, name="gwb", align_bytes=64)
+        gwc = wstage.tile([P, 4096], BF16, name="gwc", align_bytes=64)
+        wbq = const.tile([P, 1024], U32, name="wbq", align_bytes=64)
+        wbs = const.tile([P, 1024], U8, name="wbs", align_bytes=64)
+        wcq = const.tile([P, 1024], U32, name="wcq", align_bytes=64)
+        wcs = const.tile([P, 1024], U8, name="wcs", align_bytes=64)
+
+        def prep_wb(c):
+            wps = ps_ms.tile([P, 512], F32, name="wps", tag="ms")
+            words = wb_nat[:].bitcast(F32)
+            for q in range(4):
+                nc.tensor.transpose(
+                    wps[:, q * P : (q + 1) * P], words[:, c * 512 + q * P : c * 512 + (q + 1) * P], ident_f[:]
+                )
+            nc.scalar.copy(
+                out=gwb[:].bitcast(F32).rearrange("p (g c m u) -> p g c m u", g=2, c=CHUNKS, u=2)[:, :, c, :, :],
+                in_=wps[:].rearrange("p (g u m) -> p g m u", g=2, u=2),
+            )
+
+        def prep_wc(c):
+            if c % 2 == 0:
+                cps = ps_mb.tile([P, 1024], BF16, name="cps", tag="mb")
+            else:
+                cps = ps_op.tile([P, 1024], BF16, name="cps", tag="op")
+            for b in range(8):
+                nc.tensor.transpose(
+                    cps[:, b * P : (b + 1) * P], wc_nat[:, c * KDIM + b * P : c * KDIM + (b + 1) * P], ident_b[:]
+                )
+            dst = gwc[:].rearrange("p (g c m t) -> p g c m t", g=2, c=CHUNKS, t=4)[:, :, c, :, :]
+            srcv = cps[:].rearrange("p (g t m) -> p g m t", g=2, t=4)
+            if c % 2 == 0:
+                nc.scalar.copy(out=dst, in_=srcv)
+            else:
+                nc.vector.tensor_copy(out=dst, in_=srcv)
+
+        def quant_w(grouped, codes, scales):
+            nc.vector.quantize_mx(out=codes[:].bitcast(FP8X4), scales=scales[:], in_=grouped[:])
+
+        def x_of(tau):
+            return xt[tau // GROUP][:, (tau % GROUP) * KDIM : (tau % GROUP + 1) * KDIM]
+
+        def st_k(tau):
+            if tau < 0 or tau >= TILES:
+                return
+            t = kpool.tile([P, KDIM], I32, name="kint", tag="kint")
+            nc.gpsimd.tensor_scalar(
+                out=t[:], in0=x_of(tau), scalar1=cyc[:, 0:1], scalar2=0.0, op0=ALU.mult, op1=ALU.add
+            )
+            kt[tau] = t
+
+        def st_f(tau):
+            if tau < 0 or tau >= TILES:
+                return
+            t = fpool.tile([P, KDIM], F32, name="frac", tag="frac")
+            nc.vector.scalar_tensor_tensor(
+                out=t[:], in0=x_of(tau), scalar=cyc[:, 0:1], in1=kt[tau][:], op0=ALU.mult, op1=ALU.subtract
+            )
+            ft[tau] = t
+
+        def st_sin(tau):
+            if tau < 0 or tau >= TILES:
+                return
+            nc.scalar.activation(out=ft[tau][:], in_=ft[tau][:], func=ACT.Sin, scale=TWO_PI)
+
+        def st_ts(tau):
+            if tau < 0 or tau >= TILES:
+                return
+            for g in range(2):
+                ps = ps_sn.tile([P, 512], F32, name="snps", tag="sn")
+                for t in range(4):
+                    b = 4 * g + t
+                    nc.tensor.transpose(ps[:, t * P : (t + 1) * P], ft[tau][:, b * P : (b + 1) * P], ident_f[:])
+                snps[(tau, g)] = ps
+
+        def st_ex(tau):
+            if tau < 0 or tau >= TILES:
+                return
+            t = gpool.tile([P, 1024], BF16, name="gs", tag="gs", align_bytes=64)
+            for g in range(2):
+                nc.vector.tensor_tensor(
+                    out=t[:, g * 512 : (g + 1) * 512].rearrange("p (r t) -> p r t", t=4),
+                    in0=snps[(tau, g)][:].rearrange("p (t r) -> p r t", t=4),
+                    in1=vt[:, 8 + 4 * g : 12 + 4 * g].unsqueeze(1).to_broadcast([P, P, 4]),
+                    op=ALU.mult,
+                )
+            gst[tau] = t
+
+        def st_tx(tau):
+            if tau < 0 or tau >= TILES:
+                return
+            ps = ps_xt.tile([P, 512], F32, name="xps", tag="xt")
+            words = xt[tau // GROUP][:].bitcast(F32)
+            base = (tau % GROUP) * 512
+            for q in range(4):
+                nc.tensor.transpose(ps[:, q * P : (q + 1) * P], words[:, base + q * P : base + (q + 1) * P], ident_f[:])
+            xps[tau] = ps
+
+        def st_silu(tau):
+            if tau < 0 or tau >= TILES:
+                return
+            t = gpool.tile([P, 1024], BF16, name="ga", tag="ga", align_bytes=64)
+            halves = xps[tau][:].bitcast(BF16)
+            for g in range(2):
+                nc.scalar.activation(
+                    out=t[:, g * 512 : (g + 1) * 512].rearrange("p (r u e) -> p r u e", u=2, e=2),
+                    in_=halves[:, g * 512 : (g + 1) * 512].rearrange("p (u r e) -> p r u e", u=2, e=2),
+                    func=ACT.Silu,
+                )
+            gat[tau] = t
+
+        def st_quant(tau):
+            if tau < 0 or tau >= TILES:
+                return
+            grp = tau // GROUP
+            j = tau % GROUP
+            if j == 0:
+                aq[grp] = qpool.tile([P, 1024], U32, name="aq", tag="aq", align_bytes=64)
+                asc[grp] = qpool.tile([P, 1024], U8, name="asc", tag="asc", align_bytes=64)
+                sq[grp] = qpool.tile([P, 1024], U32, name="sq", tag="sq", align_bytes=64)
+                ssc[grp] = qpool.tile([P, 1024], U8, name="ssc", tag="ssc", align_bytes=64)
+            for grouped, codes, scales in ((gat[tau], aq[grp], asc[grp]), (gst[tau], sq[grp], ssc[grp])):
+                for g in range(2):
+                    cols = slice(g * 512 + j * P, g * 512 + (j + 1) * P)
+                    nc.vector.quantize_mx(
+                        out=codes[:, cols].bitcast(FP8X4),
+                        scales=scales[:, cols],
+                        in_=grouped[:, g * 512 : (g + 1) * 512],
+                    )
+
+        def st_mx(e):
+            if e < 0 or e >= TILES:
+                return
+            grp = e // CHUNKS
+            c = e % CHUNKS
+            pb = ps_mb.tile([P, 512], F32, name="bps", tag="mb")
+            pspl = ps_ms.tile([P, 512], F32, name="sps", tag="ms")
+            for acc, wq, ws, dq, ds in ((pb, wbq, wbs, aq[grp], asc[grp]), (pspl, wcq, wcs, sq[grp], ssc[grp])):
+                for g in range(2):
+                    wcols = slice(g * 512 + c * P, g * 512 + (c + 1) * P)
+                    dcols = slice(g * 512, (g + 1) * 512)
+                    nc.tensor.matmul_mx(
+                        out=acc[:],
+                        lhsT=wq[:, wcols].bitcast(FP8X4),
+                        lhsT_scale=ws[:, wcols],
+                        rhs=dq[:, dcols].bitcast(FP8X4),
+                        rhs_scale=ds[:, dcols],
+                        start=(g == 0),
+                        stop=(g == 1),
+                    )
+            bps[e] = pb
+            sps[e] = pspl
+
+        def st_a(e):
+            if e < 0 or e >= TILES:
+                return
+            c = e % CHUNKS
+            t = tbpool.tile([P, 512], F32, name="tb", tag="tb")
+            nc.scalar.activation(out=t[:], in_=bps[e][:], func=ACT.Identity, bias=spb[:, c : c + 1], scale=1.0)
+            tbt[e] = t
+
+        def st_b(e):
+            if e < 0 or e >= TILES:
+                return
+            c = e % CHUNKS
+            t = otpool.tile([P, 512], F32, name="ot", tag="ot")
+            nc.vector.scalar_tensor_tensor(
+                out=t[:], in0=sps[e][:], scalar=vt[:, c : c + 1], in1=tbt[e][:], op0=ALU.mult, op1=ALU.add
+            )
+            ott[e] = t
+
+        def st_to(e):
+            if e < 0 or e >= TILES:
+                return
+            grp = e // GROUP
+            j = e % GROUP
+            ps = ps_op.tile([P, 512], F32, name="ops", tag="op")
+            for c in range(CHUNKS):
+                nc.tensor.transpose(
+                    ps[:, c * P : (c + 1) * P], ott[grp * CHUNKS + c][:, j * P : (j + 1) * P], ident_f[:]
+                )
+            ops[e] = ps
+
+        def st_c(e):
+            if e < 0 or e >= TILES:
+                return
+            grp = e // GROUP
+            j = e % GROUP
+            if j == 0:
+                ost[grp] = ospool.tile([P, GROUP * NOUT], F32, name="osb", tag="osb")
+            nc.scalar.copy(out=ost[grp][:, j * NOUT : (j + 1) * NOUT], in_=ops[e][:])
+            if j == GROUP - 1:
+                nc.sync.dma_start(
+                    out=of[grp * 512 : (grp + 1) * 512, :].rearrange("(p j) f -> p (j f)", j=GROUP), in_=ost[grp][:]
+                )
+
+        for s in range(-5, TILES + 9):
+            st_mx(s - 4)
+            st_b(s - 5)
+            st_ex(s)
+            st_silu(s + 2)
+            st_a(s - 4)
+            st_to(s - 9)
+            st_c(s - 9)
+            st_tx(s + 3)
+            st_ts(s + 1)
+            st_sin(s + 2)
+            st_f(s + 3)
+            st_k(s + 5)
+            st_quant(s)
+            if s == 0:
+                prep_wb(0)
+                prep_wb(1)
+            if s == 1:
+                prep_wb(2)
+                prep_wb(3)
+                quant_w(gwb, wbq, wbs)
+            if s == 2:
+                prep_wc(0)
+                prep_wc(1)
+            if s == 3:
+                prep_wc(2)
+                prep_wc(3)
+                quant_w(gwc, wcq, wcs)
+            if s >= 1 and s % 4 == 1 and s // 4 + 4 < TILES // GROUP:
+                load_x(s // 4 + 4)

@@ -36,15 +36,20 @@ def tile_efficient_skan_batch_t_kernel(tc, x, base_weight, grid, scale_sp, coef,
         fpool = ctx.enter_context(tc.tile_pool(name="fpool", bufs=4))
         gpool = ctx.enter_context(tc.tile_pool(name="gpool", bufs=4))
         qpool = ctx.enter_context(tc.tile_pool(name="qpool", bufs=2))
-        tbpool = ctx.enter_context(tc.tile_pool(name="tbpool", bufs=2))
-        otpool = ctx.enter_context(tc.tile_pool(name="otpool", bufs=8))
-        ospool = ctx.enter_context(tc.tile_pool(name="ospool", bufs=2))
+        tbpool = ctx.enter_context(tc.tile_pool(name="tbpool", bufs=5))
+        otpool = ctx.enter_context(tc.tile_pool(name="otpool", bufs=6))
+        ospool = ctx.enter_context(tc.tile_pool(name="ospool", bufs=4))
         ps_xt = ctx.enter_context(tc.psum_pool(name="ps_xt", bufs=2))
         ps_sn = ctx.enter_context(tc.psum_pool(name="ps_sn", bufs=2))
         ps_mb = ctx.enter_context(tc.psum_pool(name="ps_mb", bufs=1))
         ps_ms = ctx.enter_context(tc.psum_pool(name="ps_ms", bufs=2))
         ps_op = ctx.enter_context(tc.psum_pool(name="ps_op", bufs=1))
         ctx.enter_context(tc.manual_schedule())
+
+        psum = {"xt": ps_xt, "sn": ps_sn, "mb": ps_mb, "ms": ps_ms, "op": ps_op}
+
+        def bank(kind, name, dtype=F32, cols=512):
+            return psum[kind].tile([P, cols], dtype, name=name, tag=kind)
 
         xt = {}
         kt = {}
@@ -62,7 +67,7 @@ def tile_efficient_skan_batch_t_kernel(tc, x, base_weight, grid, scale_sp, coef,
         tbt = {}
         ott = {}
         ops = {}
-        ost = {}
+        wps = {}
 
         def load_x(grp):
             t = xpool.tile([P, GROUP * KDIM], BF16, name="x_nat", tag="x_nat")
@@ -107,13 +112,6 @@ def tile_efficient_skan_batch_t_kernel(tc, x, base_weight, grid, scale_sp, coef,
         cyc = const.tile([P, 1], F32, name="cyc")
         nc.vector.tensor_scalar(out=cyc[:], in0=g_bf[:], scalar1=1.0 / TWO_PI, scalar2=None, op0=ALU.mult)
 
-        vps = ps_op.tile([P, P], BF16, name="vps", tag="op")
-        nc.tensor.transpose(vps[:], vecs[:], ident_b[:])
-        vt = const.tile([P, 16], F32, name="vt")
-        nc.vector.tensor_copy(out=vt[:], in_=vps[:, 0:16])
-        spb = const.tile([P, CHUNKS], F32, name="spb")
-        nc.vector.tensor_mul(out=spb[:], in0=vt[:, 0:4], in1=vt[:, 4:8])
-
         gwb = wstage.tile([P, 4096], BF16, name="gwb", align_bytes=64)
         gwc = wstage.tile([P, 4096], BF16, name="gwc", align_bytes=64)
         wbq = const.tile([P, 1024], U32, name="wbq", align_bytes=64)
@@ -121,33 +119,42 @@ def tile_efficient_skan_batch_t_kernel(tc, x, base_weight, grid, scale_sp, coef,
         wcq = const.tile([P, 1024], U32, name="wcq", align_bytes=64)
         wcs = const.tile([P, 1024], U8, name="wcs", align_bytes=64)
 
-        def prep_wb(c):
-            wps = ps_ms.tile([P, 512], F32, name="wps", tag="ms")
+        def copy_out(on_vector, dst, srcv):
+            if on_vector:
+                nc.vector.tensor_copy(out=dst, in_=srcv)
+            else:
+                nc.scalar.copy(out=dst, in_=srcv)
+
+        def wb_t(c, kind):
+            ps = bank(kind, "wbps")
             words = wb_nat[:].bitcast(F32)
             for q in range(4):
                 nc.tensor.transpose(
-                    wps[:, q * P : (q + 1) * P], words[:, c * 512 + q * P : c * 512 + (q + 1) * P], ident_f[:]
+                    ps[:, q * P : (q + 1) * P], words[:, c * 512 + q * P : c * 512 + (q + 1) * P], ident_f[:]
                 )
-            nc.scalar.copy(
-                out=gwb[:].bitcast(F32).rearrange("p (g c m u) -> p g c m u", g=2, c=CHUNKS, u=2)[:, :, c, :, :],
-                in_=wps[:].rearrange("p (g u m) -> p g m u", g=2, u=2),
+            wps[("b", c)] = ps
+
+        def wb_c(c, on_vector):
+            copy_out(
+                on_vector,
+                gwb[:].bitcast(F32).rearrange("p (g c m u) -> p g c m u", g=2, c=CHUNKS, u=2)[:, :, c, :, :],
+                wps[("b", c)][:].rearrange("p (g u m) -> p g m u", g=2, u=2),
             )
 
-        def prep_wc(c):
-            if c % 2 == 0:
-                cps = ps_mb.tile([P, 1024], BF16, name="cps", tag="mb")
-            else:
-                cps = ps_op.tile([P, 1024], BF16, name="cps", tag="op")
+        def wc_t(c, kind):
+            ps = bank(kind, "wcps", BF16, 1024)
             for b in range(8):
                 nc.tensor.transpose(
-                    cps[:, b * P : (b + 1) * P], wc_nat[:, c * KDIM + b * P : c * KDIM + (b + 1) * P], ident_b[:]
+                    ps[:, b * P : (b + 1) * P], wc_nat[:, c * KDIM + b * P : c * KDIM + (b + 1) * P], ident_b[:]
                 )
-            dst = gwc[:].rearrange("p (g c m t) -> p g c m t", g=2, c=CHUNKS, t=4)[:, :, c, :, :]
-            srcv = cps[:].rearrange("p (g t m) -> p g m t", g=2, t=4)
-            if c % 2 == 0:
-                nc.scalar.copy(out=dst, in_=srcv)
-            else:
-                nc.vector.tensor_copy(out=dst, in_=srcv)
+            wps[("c", c)] = ps
+
+        def wc_c(c, on_vector):
+            copy_out(
+                on_vector,
+                gwc[:].rearrange("p (g c m t) -> p g c m t", g=2, c=CHUNKS, t=4)[:, :, c, :, :],
+                wps[("c", c)][:].rearrange("p (g t m) -> p g m t", g=2, t=4),
+            )
 
         def quant_w(grouped, codes, scales):
             nc.vector.quantize_mx(out=codes[:].bitcast(FP8X4), scales=scales[:], in_=grouped[:])
@@ -155,13 +162,12 @@ def tile_efficient_skan_batch_t_kernel(tc, x, base_weight, grid, scale_sp, coef,
         def x_of(tau):
             return xt[tau // GROUP][:, (tau % GROUP) * KDIM : (tau % GROUP + 1) * KDIM]
 
-        def st_k(tau):
+        def st_k(tau, on_vector=False):
             if tau < 0 or tau >= TILES:
                 return
             t = kpool.tile([P, KDIM], I32, name="kint", tag="kint")
-            nc.gpsimd.tensor_scalar(
-                out=t[:], in0=x_of(tau), scalar1=cyc[:, 0:1], scalar2=0.0, op0=ALU.mult, op1=ALU.add
-            )
+            eng = nc.vector if on_vector else nc.gpsimd
+            eng.tensor_scalar(out=t[:], in0=x_of(tau), scalar1=cyc[:, 0:1], scalar2=0.0, op0=ALU.mult, op1=ALU.add)
             kt[tau] = t
 
         def st_f(tau):
@@ -182,7 +188,7 @@ def tile_efficient_skan_batch_t_kernel(tc, x, base_weight, grid, scale_sp, coef,
             if tau < 0 or tau >= TILES:
                 return
             for g in range(2):
-                ps = ps_sn.tile([P, 512], F32, name="snps", tag="sn")
+                ps = bank("sn", "snps")
                 for t in range(4):
                     b = 4 * g + t
                     nc.tensor.transpose(ps[:, t * P : (t + 1) * P], ft[tau][:, b * P : (b + 1) * P], ident_f[:])
@@ -204,7 +210,7 @@ def tile_efficient_skan_batch_t_kernel(tc, x, base_weight, grid, scale_sp, coef,
         def st_tx(tau):
             if tau < 0 or tau >= TILES:
                 return
-            ps = ps_xt.tile([P, 512], F32, name="xps", tag="xt")
+            ps = bank("xt", "xps")
             words = xt[tau // GROUP][:].bitcast(F32)
             base = (tau % GROUP) * 512
             for q in range(4):
@@ -224,47 +230,57 @@ def tile_efficient_skan_batch_t_kernel(tc, x, base_weight, grid, scale_sp, coef,
                 )
             gat[tau] = t
 
-        def st_quant(tau):
+        def quant_tile(tau, grouped, codes, scales):
+            j = tau % GROUP
+            for g in range(2):
+                cols = slice(g * 512 + j * P, g * 512 + (j + 1) * P)
+                nc.vector.quantize_mx(
+                    out=codes[:, cols].bitcast(FP8X4), scales=scales[:, cols], in_=grouped[:, g * 512 : (g + 1) * 512]
+                )
+
+        def st_qa(tau):
             if tau < 0 or tau >= TILES:
                 return
             grp = tau // GROUP
-            j = tau % GROUP
-            if j == 0:
+            if tau % GROUP == 0:
                 aq[grp] = qpool.tile([P, 1024], U32, name="aq", tag="aq", align_bytes=64)
                 asc[grp] = qpool.tile([P, 1024], U8, name="asc", tag="asc", align_bytes=64)
+            quant_tile(tau, gat[tau], aq[grp], asc[grp])
+
+        def st_qs(tau):
+            if tau < 0 or tau >= TILES:
+                return
+            grp = tau // GROUP
+            if tau % GROUP == 0:
                 sq[grp] = qpool.tile([P, 1024], U32, name="sq", tag="sq", align_bytes=64)
                 ssc[grp] = qpool.tile([P, 1024], U8, name="ssc", tag="ssc", align_bytes=64)
-            for grouped, codes, scales in ((gat[tau], aq[grp], asc[grp]), (gst[tau], sq[grp], ssc[grp])):
-                for g in range(2):
-                    cols = slice(g * 512 + j * P, g * 512 + (j + 1) * P)
-                    nc.vector.quantize_mx(
-                        out=codes[:, cols].bitcast(FP8X4),
-                        scales=scales[:, cols],
-                        in_=grouped[:, g * 512 : (g + 1) * 512],
-                    )
+            quant_tile(tau, gst[tau], sq[grp], ssc[grp])
 
-        def st_mx(e):
+        def mx_group(acc, c, wq, ws, dq, dsc):
+            for g in range(2):
+                wcols = slice(g * 512 + c * P, g * 512 + (c + 1) * P)
+                dcols = slice(g * 512, (g + 1) * 512)
+                nc.tensor.matmul_mx(
+                    out=acc[:],
+                    lhsT=wq[:, wcols].bitcast(FP8X4),
+                    lhsT_scale=ws[:, wcols],
+                    rhs=dq[:, dcols].bitcast(FP8X4),
+                    rhs_scale=dsc[:, dcols],
+                    start=(g == 0),
+                    stop=(g == 1),
+                )
+
+        def st_mxb(e, kind="mb"):
             if e < 0 or e >= TILES:
                 return
-            grp = e // CHUNKS
-            c = e % CHUNKS
-            pb = ps_mb.tile([P, 512], F32, name="bps", tag="mb")
-            pspl = ps_ms.tile([P, 512], F32, name="sps", tag="ms")
-            for acc, wq, ws, dq, ds in ((pb, wbq, wbs, aq[grp], asc[grp]), (pspl, wcq, wcs, sq[grp], ssc[grp])):
-                for g in range(2):
-                    wcols = slice(g * 512 + c * P, g * 512 + (c + 1) * P)
-                    dcols = slice(g * 512, (g + 1) * 512)
-                    nc.tensor.matmul_mx(
-                        out=acc[:],
-                        lhsT=wq[:, wcols].bitcast(FP8X4),
-                        lhsT_scale=ws[:, wcols],
-                        rhs=dq[:, dcols].bitcast(FP8X4),
-                        rhs_scale=ds[:, dcols],
-                        start=(g == 0),
-                        stop=(g == 1),
-                    )
-            bps[e] = pb
-            sps[e] = pspl
+            bps[e] = bank(kind, "bps")
+            mx_group(bps[e], e % CHUNKS, wbq, wbs, aq[e // CHUNKS], asc[e // CHUNKS])
+
+        def st_mxs(e, kind="ms"):
+            if e < 0 or e >= TILES:
+                return
+            sps[e] = bank(kind, "sps")
+            mx_group(sps[e], e % CHUNKS, wcq, wcs, sq[e // CHUNKS], ssc[e // CHUNKS])
 
         def st_a(e):
             if e < 0 or e >= TILES:
@@ -284,58 +300,103 @@ def tile_efficient_skan_batch_t_kernel(tc, x, base_weight, grid, scale_sp, coef,
             )
             ott[e] = t
 
-        def st_to(e):
+        def st_to(e, kind="op"):
             if e < 0 or e >= TILES:
                 return
-            grp = e // GROUP
-            j = e % GROUP
-            ps = ps_op.tile([P, 512], F32, name="ops", tag="op")
-            for c in range(CHUNKS):
-                nc.tensor.transpose(
-                    ps[:, c * P : (c + 1) * P], ott[grp * CHUNKS + c][:, j * P : (j + 1) * P], ident_f[:]
-                )
+            ps = bank(kind, "ops")
+            for j in range(GROUP):
+                nc.tensor.transpose(ps[:, j * P : (j + 1) * P], ott[e][:, j * P : (j + 1) * P], ident_f[:])
             ops[e] = ps
 
-        def st_c(e):
+        def st_c(e, on_vector=False):
             if e < 0 or e >= TILES:
                 return
-            grp = e // GROUP
-            j = e % GROUP
-            if j == 0:
-                ost[grp] = ospool.tile([P, GROUP * NOUT], F32, name="osb", tag="osb")
-            nc.scalar.copy(out=ost[grp][:, j * NOUT : (j + 1) * NOUT], in_=ops[e][:])
-            if j == GROUP - 1:
-                nc.sync.dma_start(
-                    out=of[grp * 512 : (grp + 1) * 512, :].rearrange("(p j) f -> p (j f)", j=GROUP), in_=ost[grp][:]
-                )
+            grp = e // CHUNKS
+            c = e % CHUNKS
+            t = ospool.tile([P, 512], F32, name="osb", tag="osb")
+            copy_out(on_vector, t[:], ops[e][:])
+            nc.sync.dma_start(
+                out=of[grp * 512 : (grp + 1) * 512, :].rearrange("(p j) f -> p j f", j=GROUP)[:, :, c * P : (c + 1) * P],
+                in_=t[:].rearrange("p (j f) -> p j f", j=GROUP),
+            )
 
-        for s in range(-5, TILES + 9):
-            st_mx(s - 4)
+        st_k(0, True)
+        vps = bank("op", "vps", BF16, P)
+        nc.tensor.transpose(vps[:], vecs[:], ident_b[:])
+        vt = const.tile([P, 16], F32, name="vt")
+        nc.vector.tensor_copy(out=vt[:], in_=vps[:, 0:16])
+        spb = const.tile([P, CHUNKS], F32, name="spb")
+        nc.vector.tensor_mul(out=spb[:], in0=vt[:, 0:4], in1=vt[:, 4:8])
+
+        for s in range(-5, TILES):
+            st_mxb(s - 4)
+            st_mxs(s - 4)
             st_b(s - 5)
             st_ex(s)
             st_silu(s + 2)
             st_a(s - 4)
-            st_to(s - 9)
-            st_c(s - 9)
+            st_to(s - 6)
+            st_c(s - 6)
             st_tx(s + 3)
             st_ts(s + 1)
             st_sin(s + 2)
             st_f(s + 3)
-            st_k(s + 5)
-            st_quant(s)
+            if s + 5 != 0:
+                st_k(s + 5)
+            st_qa(s + 1)
+            st_qs(s)
+            if s == -1:
+                wb_t(0, "ms")
+                wb_t(1, "ms")
+                wb_t(2, "mb")
             if s == 0:
-                prep_wb(0)
-                prep_wb(1)
+                wb_c(0, False)
+                wb_c(1, False)
+                wb_c(2, True)
+                wb_t(3, "ms")
+                wc_t(0, "ms")
             if s == 1:
-                prep_wb(2)
-                prep_wb(3)
+                wb_c(3, False)
+                wc_c(0, False)
                 quant_w(gwb, wbq, wbs)
+                wc_t(1, "mb")
+                wc_t(2, "ms")
             if s == 2:
-                prep_wc(0)
-                prep_wc(1)
+                wc_c(1, True)
+                wc_c(2, False)
+                wc_t(3, "ms")
             if s == 3:
-                prep_wc(2)
-                prep_wc(3)
+                wc_c(3, False)
                 quant_w(gwc, wcq, wcs)
             if s >= 1 and s % 4 == 1 and s // 4 + 4 < TILES // GROUP:
                 load_x(s // 4 + 4)
+
+        st_mxb(28, "mb")
+        st_mxb(29, "xt")
+        st_mxb(30, "xt")
+        st_a(28)
+        st_a(29)
+        st_a(30)
+        st_mxb(31, "mb")
+        st_a(31)
+        st_to(26, "op")
+        st_c(26)
+        st_b(27)
+        st_mxs(28, "ms")
+        st_mxs(29, "ms")
+        st_mxs(30, "sn")
+        st_mxs(31, "sn")
+        st_b(28)
+        st_b(29)
+        st_b(30)
+        st_b(31)
+        st_to(27, "op")
+        st_c(27)
+        st_to(28, "mb")
+        st_c(28)
+        st_to(29, "xt")
+        st_c(29)
+        st_to(30, "xt")
+        st_c(30)
+        st_to(31, "ms")
+        st_c(31, True)

@@ -44,7 +44,6 @@ def tile_efficient_skan_batch_t_kernel(tc, x, base_weight, grid, scale_sp, coef,
         ps_mb = ctx.enter_context(tc.psum_pool(name="ps_mb", bufs=1))
         ps_ms = ctx.enter_context(tc.psum_pool(name="ps_ms", bufs=2))
         ps_op = ctx.enter_context(tc.psum_pool(name="ps_op", bufs=1))
-        ctx.enter_context(tc.manual_schedule())
 
         psum = {"xt": ps_xt, "sn": ps_sn, "mb": ps_mb, "ms": ps_ms, "op": ps_op}
 

@@ -44,6 +44,7 @@ def tile_efficient_skan_batch_t_kernel(tc, x, base_weight, grid, scale_sp, coef,
         ps_mb = ctx.enter_context(tc.psum_pool(name="ps_mb", bufs=1))
         ps_ms = ctx.enter_context(tc.psum_pool(name="ps_ms", bufs=2))
         ps_op = ctx.enter_context(tc.psum_pool(name="ps_op", bufs=1))
+        ctx.enter_context(tc.manual_schedule())
 
         psum = {"xt": ps_xt, "sn": ps_sn, "mb": ps_mb, "ms": ps_ms, "op": ps_op}
 
@@ -213,20 +214,21 @@ def tile_efficient_skan_batch_t_kernel(tc, x, base_weight, grid, scale_sp, coef,
             words = xt[tau // GROUP][:].bitcast(F32)
             base = (tau % GROUP) * 512
             for q in range(4):
-                nc.tensor.transpose(ps[:, q * P : (q + 1) * P], words[:, base + q * P : base + (q + 1) * P], ident_f[:])
+                place = 2 * (q % 2) + q // 2
+                nc.tensor.transpose(
+                    ps[:, place * P : (place + 1) * P], words[:, base + q * P : base + (q + 1) * P], ident_f[:]
+                )
             xps[tau] = ps
 
         def st_silu(tau):
             if tau < 0 or tau >= TILES:
                 return
             t = gpool.tile([P, 1024], BF16, name="ga", tag="ga", align_bytes=64)
-            halves = xps[tau][:].bitcast(BF16)
-            for g in range(2):
-                nc.scalar.activation(
-                    out=t[:, g * 512 : (g + 1) * 512].rearrange("p (r u e) -> p r u e", u=2, e=2),
-                    in_=halves[:, g * 512 : (g + 1) * 512].rearrange("p (u r e) -> p r u e", u=2, e=2),
-                    func=ACT.Silu,
-                )
+            nc.scalar.activation(
+                out=t[:].rearrange("p (x u e) -> p x u e", u=2, e=2),
+                in_=xps[tau][:].bitcast(BF16).rearrange("p (u x e) -> p x u e", u=2, e=2),
+                func=ACT.Silu,
+            )
             gat[tau] = t
 
         def quant_tile(tau, grouped, codes, scales):

@@ -331,7 +331,6 @@ def tile_efficient_skan_batch_t_kernel(tc, x, base_weight, grid, scale_sp, coef,
 
         for s in range(-5, TILES):
             st_mxb(s - 4)
-            st_mxs(s - 4)
             st_b(s - 5)
             st_ex(s)
             st_silu(s + 2)
@@ -339,6 +338,7 @@ def tile_efficient_skan_batch_t_kernel(tc, x, base_weight, grid, scale_sp, coef,
             st_to(s - 6)
             st_c(s - 6)
             st_tx(s + 3)
+            st_mxs(s - 4)
             st_ts(s + 1)
             st_sin(s + 2)
             st_f(s + 3)

@@ -331,8 +331,8 @@ def tile_efficient_skan_batch_t_kernel(tc, x, base_weight, grid, scale_sp, coef,
 
         for s in range(-5, TILES):
             st_mxb(s - 4)
-            st_b(s - 5)
             st_ex(s)
+            st_b(s - 5)
             st_silu(s + 2)
             st_a(s - 4)
             st_to(s - 6)
@@ -341,11 +341,11 @@ def tile_efficient_skan_batch_t_kernel(tc, x, base_weight, grid, scale_sp, coef,
             st_mxs(s - 4)
             st_ts(s + 1)
             st_sin(s + 2)
-            st_f(s + 3)
             if s + 5 != 0:
                 st_k(s + 5)
             st_qa(s + 1)
             st_qs(s)
+            st_f(s + 3)
             if s == -1:
                 wb_t(0, "ms")
                 wb_t(1, "ms")

@@ -17,6 +17,7 @@ ALU = mybir.AluOpType
 ACT = mybir.ActivationFunctionType
 
 TILES = 32
+HALF0 = 28
 GROUP = 4
 CHUNKS = 4
 KDIM = 1024
@@ -35,7 +36,7 @@ def tile_efficient_skan_batch_t_kernel(tc, x, base_weight, grid, scale_sp, coef,
         kpool = ctx.enter_context(tc.tile_pool(name="kpool", bufs=3))
         fpool = ctx.enter_context(tc.tile_pool(name="fpool", bufs=4))
         gpool = ctx.enter_context(tc.tile_pool(name="gpool", bufs=4))
-        qpool = ctx.enter_context(tc.tile_pool(name="qpool", bufs=2))
+        qpool = ctx.enter_context(tc.tile_pool(name="qpool", bufs=3))
         tbpool = ctx.enter_context(tc.tile_pool(name="tbpool", bufs=5))
         otpool = ctx.enter_context(tc.tile_pool(name="otpool", bufs=6))
         ospool = ctx.enter_context(tc.tile_pool(name="ospool", bufs=4))
@@ -231,10 +232,15 @@ def tile_efficient_skan_batch_t_kernel(tc, x, base_weight, grid, scale_sp, coef,
             )
             gat[tau] = t
 
+        def operand_of(tau):
+            if tau < HALF0:
+                return tau // GROUP, tau % GROUP, GROUP
+            return HALF0 // GROUP + (tau - HALF0) // 2, tau % 2, 2
+
         def quant_tile(tau, grouped, codes, scales):
-            j = tau % GROUP
+            key, j, w = operand_of(tau)
             for g in range(2):
-                cols = slice(g * 512 + j * P, g * 512 + (j + 1) * P)
+                cols = slice((g * w + j) * P, (g * w + j + 1) * P)
                 nc.vector.quantize_mx(
                     out=codes[:, cols].bitcast(FP8X4), scales=scales[:, cols], in_=grouped[:, g * 512 : (g + 1) * 512]
                 )
@@ -242,20 +248,20 @@ def tile_efficient_skan_batch_t_kernel(tc, x, base_weight, grid, scale_sp, coef,
         def st_qa(tau):
             if tau < 0 or tau >= TILES:
                 return
-            grp = tau // GROUP
-            if tau % GROUP == 0:
-                aq[grp] = qpool.tile([P, 1024], U32, name="aq", tag="aq", align_bytes=64)
-                asc[grp] = qpool.tile([P, 1024], U8, name="asc", tag="asc", align_bytes=64)
-            quant_tile(tau, gat[tau], aq[grp], asc[grp])
+            key, j, w = operand_of(tau)
+            if j == 0:
+                aq[key] = qpool.tile([P, 1024], U32, name="aq", tag="aq", align_bytes=64)
+                asc[key] = qpool.tile([P, 1024], U8, name="asc", tag="asc", align_bytes=64)
+            quant_tile(tau, gat[tau], aq[key], asc[key])
 
         def st_qs(tau):
             if tau < 0 or tau >= TILES:
                 return
-            grp = tau // GROUP
-            if tau % GROUP == 0:
-                sq[grp] = qpool.tile([P, 1024], U32, name="sq", tag="sq", align_bytes=64)
-                ssc[grp] = qpool.tile([P, 1024], U8, name="ssc", tag="ssc", align_bytes=64)
-            quant_tile(tau, gst[tau], sq[grp], ssc[grp])
+            key, j, w = operand_of(tau)
+            if j == 0:
+                sq[key] = qpool.tile([P, 1024], U32, name="sq", tag="sq", align_bytes=64)
+                ssc[key] = qpool.tile([P, 1024], U8, name="ssc", tag="ssc", align_bytes=64)
+            quant_tile(tau, gst[tau], sq[key], ssc[key])
 
         def mx_group(acc, c, wq, ws, dq, dsc):
             for g in range(2):
@@ -272,19 +278,19 @@ def tile_efficient_skan_batch_t_kernel(tc, x, base_weight, grid, scale_sp, coef,
                 )
 
         def st_mxb(e, kind="mb"):
-            if e < 0 or e >= TILES:
+            if e < 0 or e >= HALF0:
                 return
             bps[e] = bank(kind, "bps")
             mx_group(bps[e], e % CHUNKS, wbq, wbs, aq[e // CHUNKS], asc[e // CHUNKS])
 
         def st_mxs(e, kind="ms"):
-            if e < 0 or e >= TILES:
+            if e < 0 or e >= HALF0:
                 return
             sps[e] = bank(kind, "sps")
             mx_group(sps[e], e % CHUNKS, wcq, wcs, sq[e // CHUNKS], ssc[e // CHUNKS])
 
         def st_a(e):
-            if e < 0 or e >= TILES:
+            if e < 0 or e >= HALF0:
                 return
             c = e % CHUNKS
             t = tbpool.tile([P, 512], F32, name="tb", tag="tb")
@@ -292,7 +298,7 @@ def tile_efficient_skan_batch_t_kernel(tc, x, base_weight, grid, scale_sp, coef,
             tbt[e] = t
 
         def st_b(e):
-            if e < 0 or e >= TILES:
+            if e < 0 or e >= HALF0:
                 return
             c = e % CHUNKS
             t = otpool.tile([P, 512], F32, name="ot", tag="ot")
@@ -302,7 +308,7 @@ def tile_efficient_skan_batch_t_kernel(tc, x, base_weight, grid, scale_sp, coef,
             ott[e] = t
 
         def st_to(e, kind="op"):
-            if e < 0 or e >= TILES:
+            if e < 0 or e >= HALF0:
                 return
             ps = bank(kind, "ops")
             for j in range(GROUP):
@@ -310,7 +316,7 @@ def tile_efficient_skan_batch_t_kernel(tc, x, base_weight, grid, scale_sp, coef,
             ops[e] = ps
 
         def st_c(e, on_vector=False):
-            if e < 0 or e >= TILES:
+            if e < 0 or e >= HALF0:
                 return
             grp = e // CHUNKS
             c = e % CHUNKS
@@ -319,6 +325,84 @@ def tile_efficient_skan_batch_t_kernel(tc, x, base_weight, grid, scale_sp, coef,
             nc.sync.dma_start(
                 out=of[grp * 512 : (grp + 1) * 512, :].rearrange("(p j) f -> p j f", j=GROUP)[:, :, c * P : (c + 1) * P],
                 in_=t[:].rearrange("p (j f) -> p j f", j=GROUP),
+            )
+
+        hb = {}
+        hs = {}
+        htb = {}
+        hot = {}
+        hps = {}
+
+        def half_mx(h, pc, wq, ws, dq, dsc, kind):
+            acc = bank(kind, "hacc")
+            for ci in range(2):
+                c = 2 * pc + ci
+                for g in range(2):
+                    wcols = slice(g * 512 + c * P, g * 512 + (c + 1) * P)
+                    dcols = slice(g * 256, (g + 1) * 256)
+                    nc.tensor.matmul_mx(
+                        out=acc[:, ci * 256 : (ci + 1) * 256],
+                        lhsT=wq[:, wcols].bitcast(FP8X4),
+                        lhsT_scale=ws[:, wcols],
+                        rhs=dq[:, dcols].bitcast(FP8X4),
+                        rhs_scale=dsc[:, dcols],
+                        start=(g == 0),
+                        stop=(g == 1),
+                    )
+            return acc
+
+        def half_mxb(h, pc, kind):
+            key = HALF0 // GROUP + h
+            hb[(h, pc)] = half_mx(h, pc, wbq, wbs, aq[key], asc[key], kind)
+
+        def half_mxs(h, pc, kind):
+            key = HALF0 // GROUP + h
+            hs[(h, pc)] = half_mx(h, pc, wcq, wcs, sq[key], ssc[key], kind)
+
+        def half_a(h, pc):
+            t = tbpool.tile([P, 512], F32, name="tb", tag="tb")
+            for ci in range(2):
+                c = 2 * pc + ci
+                cols = slice(ci * 256, (ci + 1) * 256)
+                nc.scalar.activation(
+                    out=t[:, cols], in_=hb[(h, pc)][:, cols], func=ACT.Identity, bias=spb[:, c : c + 1], scale=1.0
+                )
+            htb[(h, pc)] = t
+
+        def half_b(h, pc):
+            t = otpool.tile([P, 512], F32, name="ot", tag="ot")
+            for ci in range(2):
+                c = 2 * pc + ci
+                cols = slice(ci * 256, (ci + 1) * 256)
+                nc.vector.scalar_tensor_tensor(
+                    out=t[:, cols],
+                    in0=hs[(h, pc)][:, cols],
+                    scalar=vt[:, c : c + 1],
+                    in1=htb[(h, pc)][:, cols],
+                    op0=ALU.mult,
+                    op1=ALU.add,
+                )
+            hot[(h, pc)] = t
+
+        def half_to(h, pc, kind):
+            ps = bank(kind, "hps")
+            for ci in range(2):
+                for j in range(2):
+                    nc.tensor.transpose(
+                        ps[:, j * 256 + ci * P : j * 256 + (ci + 1) * P],
+                        hot[(h, pc)][:, ci * 256 + j * P : ci * 256 + (j + 1) * P],
+                        ident_f[:],
+                    )
+            hps[(h, pc)] = ps
+
+        def half_c(h, pc, on_vector=False):
+            t = ospool.tile([P, 512], F32, name="osb", tag="osb")
+            copy_out(on_vector, t[:], hps[(h, pc)][:])
+            nc.sync.dma_start(
+                out=of[HALF0 * P : TILES * P, :].rearrange("(p j) f -> p j f", j=GROUP)[
+                    :, 2 * h : 2 * h + 2, pc * 256 : (pc + 1) * 256
+                ],
+                in_=t[:].rearrange("p (j f) -> p j f", j=2),
             )
 
         st_k(0, True)
@@ -372,32 +456,34 @@ def tile_efficient_skan_batch_t_kernel(tc, x, base_weight, grid, scale_sp, coef,
             if s >= 1 and s % 4 == 1 and s // 4 + 4 < TILES // GROUP:
                 load_x(s // 4 + 4)
 
-        st_mxb(28, "mb")
-        st_mxb(29, "xt")
-        st_mxb(30, "xt")
-        st_a(28)
-        st_a(29)
-        st_a(30)
-        st_mxb(31, "mb")
-        st_a(31)
-        st_to(26, "op")
-        st_c(26)
+            if s == 30:
+                half_mxb(0, 0, "xt")
+                half_mxb(0, 1, "xt")
+                half_a(0, 0)
+                half_a(0, 1)
+
+        half_mxb(1, 0, "xt")
+        half_mxb(1, 1, "xt")
+        half_a(1, 0)
+        half_a(1, 1)
         st_b(27)
-        st_mxs(28, "ms")
-        st_mxs(29, "ms")
-        st_mxs(30, "sn")
-        st_mxs(31, "sn")
-        st_b(28)
-        st_b(29)
-        st_b(30)
-        st_b(31)
-        st_to(27, "op")
+        half_mxs(0, 0, "ms")
+        st_to(26)
+        st_c(26)
+        half_mxs(0, 1, "mb")
+        half_mxs(1, 0, "sn")
+        half_mxs(1, 1, "sn")
+        half_b(0, 0)
+        half_b(0, 1)
+        half_b(1, 0)
+        half_b(1, 1)
+        st_to(27, "ms")
         st_c(27)
-        st_to(28, "mb")
-        st_c(28)
-        st_to(29, "xt")
-        st_c(29)
-        st_to(30, "xt")
-        st_c(30)
-        st_to(31, "ms")
-        st_c(31, True)
+        half_to(0, 0, "op")
+        half_c(0, 0)
+        half_to(0, 1, "xt")
+        half_c(0, 1)
+        half_to(1, 0, "xt")
+        half_c(1, 0)
+        half_to(1, 1, "mb")
+        half_c(1, 1, True)

@@ -33,13 +33,13 @@ def tile_efficient_skan_batch_t_kernel(tc, x, base_weight, grid, scale_sp, coef,
         const = ctx.enter_context(tc.tile_pool(name="const", bufs=1))
         wstage = ctx.enter_context(tc.tile_pool(name="wstage", bufs=1))
         xpool = ctx.enter_context(tc.tile_pool(name="xpool", bufs=4))
-        kpool = ctx.enter_context(tc.tile_pool(name="kpool", bufs=3))
+        kpool = ctx.enter_context(tc.tile_pool(name="kpool", bufs=2))
         fpool = ctx.enter_context(tc.tile_pool(name="fpool", bufs=4))
         gpool = ctx.enter_context(tc.tile_pool(name="gpool", bufs=4))
         qpool = ctx.enter_context(tc.tile_pool(name="qpool", bufs=3))
         tbpool = ctx.enter_context(tc.tile_pool(name="tbpool", bufs=5))
         otpool = ctx.enter_context(tc.tile_pool(name="otpool", bufs=6))
-        ospool = ctx.enter_context(tc.tile_pool(name="ospool", bufs=4))
+        ospool = ctx.enter_context(tc.tile_pool(name="ospool", bufs=8))
         ps_xt = ctx.enter_context(tc.psum_pool(name="ps_xt", bufs=2))
         ps_sn = ctx.enter_context(tc.psum_pool(name="ps_sn", bufs=2))
         ps_mb = ctx.enter_context(tc.psum_pool(name="ps_mb", bufs=1))
@@ -406,14 +406,18 @@ def tile_efficient_skan_batch_t_kernel(tc, x, base_weight, grid, scale_sp, coef,
             )
 
         st_k(0, True)
+        st_k(1, True)
+        st_f(0)
+        st_f(1)
+        st_k(2, True)
         vps = bank("op", "vps", BF16, P)
         nc.tensor.transpose(vps[:], vecs[:], ident_b[:])
         vt = const.tile([P, 16], F32, name="vt")
         nc.vector.tensor_copy(out=vt[:], in_=vps[:, 0:16])
         spb = const.tile([P, CHUNKS], F32, name="spb")
-        nc.vector.tensor_mul(out=spb[:], in0=vt[:, 0:4], in1=vt[:, 4:8])
+        nc.vector.tensor_tensor(out=spb[:], in0=vps[:, 4:8], in1=vt[:, 0:4], op=ALU.mult)
 
-        for s in range(-5, TILES):
+        for s in range(-5, 30):
             st_mxb(s - 4)
             st_ex(s)
             st_b(s - 5)
@@ -425,11 +429,12 @@ def tile_efficient_skan_batch_t_kernel(tc, x, base_weight, grid, scale_sp, coef,
             st_mxs(s - 4)
             st_ts(s + 1)
             st_sin(s + 2)
-            if s + 5 != 0:
-                st_k(s + 5)
             st_qa(s + 1)
             st_qs(s)
-            st_f(s + 3)
+            if s + 3 >= 2:
+                st_f(s + 3)
+            if s + 5 >= 3:
+                st_k(s + 5)
             if s == -1:
                 wb_t(0, "ms")
                 wb_t(1, "ms")
@@ -437,7 +442,7 @@ def tile_efficient_skan_batch_t_kernel(tc, x, base_weight, grid, scale_sp, coef,
             if s == 0:
                 wb_c(0, False)
                 wb_c(1, False)
-                wb_c(2, True)
+                wb_c(2, False)
                 wb_t(3, "ms")
                 wc_t(0, "ms")
             if s == 1:
@@ -456,23 +461,40 @@ def tile_efficient_skan_batch_t_kernel(tc, x, base_weight, grid, scale_sp, coef,
             if s >= 1 and s % 4 == 1 and s // 4 + 4 < TILES // GROUP:
                 load_x(s // 4 + 4)
 
-            if s == 30:
-                half_mxb(0, 0, "xt")
-                half_mxb(0, 1, "xt")
-                half_a(0, 0)
-                half_a(0, 1)
 
+        st_mxb(26)
+        st_ex(30)
+        st_b(25)
+        st_a(26)
+        st_qa(31)
+        st_qs(30)
+        st_to(24)
+        st_mxs(26)
+        half_mxb(0, 0, "xt")
+        half_a(0, 0)
+        st_c(24)
+        st_ts(31)
+        st_mxb(27)
+        half_mxb(0, 1, "xt")
+        st_a(27)
+        half_a(0, 1)
+        st_ex(31)
+        st_b(26)
+        st_qs(31)
+        st_to(25)
+        st_c(25)
+        st_mxs(27)
+        half_mxs(0, 0, "ms")
+        half_mxs(0, 1, "mb")
         half_mxb(1, 0, "xt")
         half_mxb(1, 1, "xt")
         half_a(1, 0)
         half_a(1, 1)
-        st_b(27)
-        half_mxs(0, 0, "ms")
         st_to(26)
         st_c(26)
-        half_mxs(0, 1, "mb")
         half_mxs(1, 0, "sn")
         half_mxs(1, 1, "sn")
+        st_b(27)
         half_b(0, 0)
         half_b(0, 1)
         half_b(1, 0)
@@ -482,7 +504,7 @@ def tile_efficient_skan_batch_t_kernel(tc, x, base_weight, grid, scale_sp, coef,
         half_to(0, 0, "op")
         half_c(0, 0)
         half_to(0, 1, "xt")
-        half_c(0, 1)
+        half_c(0, 1, True)
         half_to(1, 0, "xt")
         half_c(1, 0)
         half_to(1, 1, "mb")

@@ -35,7 +35,7 @@ def tile_efficient_skan_batch_t_kernel(tc, x, base_weight, grid, scale_sp, coef,
         xpool = ctx.enter_context(tc.tile_pool(name="xpool", bufs=4))
         kpool = ctx.enter_context(tc.tile_pool(name="kpool", bufs=2))
         fpool = ctx.enter_context(tc.tile_pool(name="fpool", bufs=4))
-        gpool = ctx.enter_context(tc.tile_pool(name="gpool", bufs=4))
+        gpool = ctx.enter_context(tc.tile_pool(name="gpool", bufs=3))
         qpool = ctx.enter_context(tc.tile_pool(name="qpool", bufs=3))
         tbpool = ctx.enter_context(tc.tile_pool(name="tbpool", bufs=5))
         otpool = ctx.enter_context(tc.tile_pool(name="otpool", bufs=6))
@@ -86,10 +86,10 @@ def tile_efficient_skan_batch_t_kernel(tc, x, base_weight, grid, scale_sp, coef,
         vecs = const.tile([P, P], BF16, name="vecs")
         nc.vector.memset(vecs[:], 0.0)
         g_bf = const.tile([P, 1], BF16, name="g_bf")
-        nc.sync.dma_start(out=g_bf[:], in_=grid.partition_broadcast(P))
-        nc.sync.dma_start(out=vecs[0:4, :], in_=scale_sp.rearrange("(a p) -> a p", p=P))
-        nc.sync.dma_start(out=vecs[4:8, :], in_=conv_b.rearrange("o (a p) -> (o a) p", p=P))
-        nc.sync.dma_start(out=vecs[8:16, :], in_=coef.rearrange("(a p) o -> a (p o)", p=P))
+        nc.scalar.dma_start(out=g_bf[:], in_=grid.partition_broadcast(P))
+        nc.scalar.dma_start(out=vecs[0:4, :], in_=scale_sp.rearrange("(a p) -> a p", p=P))
+        nc.scalar.dma_start(out=vecs[4:8, :], in_=conv_b.rearrange("o (a p) -> (o a) p", p=P))
+        nc.scalar.dma_start(out=vecs[8:16, :], in_=coef.rearrange("(a p) o -> a (p o)", p=P))
         load_x(0)
         wb_nat = wstage.tile([P, CHUNKS * KDIM], BF16, name="wb_nat")
         nc.sync.dma_start(
@@ -198,15 +198,17 @@ def tile_efficient_skan_batch_t_kernel(tc, x, base_weight, grid, scale_sp, coef,
         def st_ex(tau):
             if tau < 0 or tau >= TILES:
                 return
-            t = gpool.tile([P, 1024], BF16, name="gs", tag="gs", align_bytes=64)
+            i = tau % 2
+            if i == 0:
+                gst[tau // 2] = gpool.tile([P, 2048], BF16, name="gs", tag="gs", align_bytes=64)
+            t = gst[tau // 2]
             for g in range(2):
                 nc.vector.tensor_tensor(
-                    out=t[:, g * 512 : (g + 1) * 512].rearrange("p (r t) -> p r t", t=4),
+                    out=t[:, g * 1024 + i * 512 : g * 1024 + (i + 1) * 512].rearrange("p (r t) -> p r t", t=4),
                     in0=snps[(tau, g)][:].rearrange("p (t r) -> p r t", t=4),
                     in1=vt[:, 8 + 4 * g : 12 + 4 * g].unsqueeze(1).to_broadcast([P, P, 4]),
                     op=ALU.mult,
                 )
-            gst[tau] = t
 
         def st_tx(tau):
             if tau < 0 or tau >= TILES:
@@ -224,44 +226,45 @@ def tile_efficient_skan_batch_t_kernel(tc, x, base_weight, grid, scale_sp, coef,
         def st_silu(tau):
             if tau < 0 or tau >= TILES:
                 return
-            t = gpool.tile([P, 1024], BF16, name="ga", tag="ga", align_bytes=64)
+            i = tau % 2
+            if i == 0:
+                gat[tau // 2] = gpool.tile([P, 2048], BF16, name="ga", tag="ga", align_bytes=64)
             nc.scalar.activation(
-                out=t[:].rearrange("p (x u e) -> p x u e", u=2, e=2),
-                in_=xps[tau][:].bitcast(BF16).rearrange("p (u x e) -> p x u e", u=2, e=2),
+                out=gat[tau // 2][:].rearrange("p (g i r u e) -> p g i r u e", g=2, i=2, u=2, e=2)[:, :, i],
+                in_=xps[tau][:].bitcast(BF16).rearrange("p (u g r e) -> p g r u e", u=2, g=2, e=2),
                 func=ACT.Silu,
             )
-            gat[tau] = t
 
-        def operand_of(tau):
-            if tau < HALF0:
-                return tau // GROUP, tau % GROUP, GROUP
-            return HALF0 // GROUP + (tau - HALF0) // 2, tau % 2, 2
+        def operand_of(pair):
+            if pair < HALF0 // 2:
+                return pair // 2, pair % 2, 2
+            return HALF0 // GROUP + pair - HALF0 // 2, 0, 1
 
-        def quant_tile(tau, grouped, codes, scales):
-            key, j, w = operand_of(tau)
+        def quant_pair(pair, grouped, codes, scales):
+            key, place, w = operand_of(pair)
             for g in range(2):
-                cols = slice((g * w + j) * P, (g * w + j + 1) * P)
+                cols = slice((g * w + place) * 256, (g * w + place + 1) * 256)
                 nc.vector.quantize_mx(
-                    out=codes[:, cols].bitcast(FP8X4), scales=scales[:, cols], in_=grouped[:, g * 512 : (g + 1) * 512]
+                    out=codes[:, cols].bitcast(FP8X4), scales=scales[:, cols], in_=grouped[:, g * 1024 : (g + 1) * 1024]
                 )
 
-        def st_qa(tau):
-            if tau < 0 or tau >= TILES:
+        def st_qa(pair):
+            if pair < 0 or pair >= TILES // 2:
                 return
-            key, j, w = operand_of(tau)
-            if j == 0:
+            key, place, w = operand_of(pair)
+            if place == 0:
                 aq[key] = qpool.tile([P, 1024], U32, name="aq", tag="aq", align_bytes=64)
                 asc[key] = qpool.tile([P, 1024], U8, name="asc", tag="asc", align_bytes=64)
-            quant_tile(tau, gat[tau], aq[key], asc[key])
+            quant_pair(pair, gat[pair], aq[key], asc[key])
 
-        def st_qs(tau):
-            if tau < 0 or tau >= TILES:
+        def st_qs(pair):
+            if pair < 0 or pair >= TILES // 2:
                 return
-            key, j, w = operand_of(tau)
-            if j == 0:
+            key, place, w = operand_of(pair)
+            if place == 0:
                 sq[key] = qpool.tile([P, 1024], U32, name="sq", tag="sq", align_bytes=64)
                 ssc[key] = qpool.tile([P, 1024], U8, name="ssc", tag="ssc", align_bytes=64)
-            quant_tile(tau, gst[tau], sq[key], ssc[key])
+            quant_pair(pair, gst[pair], sq[key], ssc[key])
 
         def mx_group(acc, c, wq, ws, dq, dsc):
             for g in range(2):
@@ -410,6 +413,7 @@ def tile_efficient_skan_batch_t_kernel(tc, x, base_weight, grid, scale_sp, coef,
         st_f(0)
         st_f(1)
         st_k(2, True)
+        st_k(3, True)
         vps = bank("op", "vps", BF16, P)
         nc.tensor.transpose(vps[:], vecs[:], ident_b[:])
         vt = const.tile([P, 16], F32, name="vt")
@@ -429,11 +433,18 @@ def tile_efficient_skan_batch_t_kernel(tc, x, base_weight, grid, scale_sp, coef,
             st_mxs(s - 4)
             st_ts(s + 1)
             st_sin(s + 2)
-            st_qa(s + 1)
-            st_qs(s)
+            if s % 2 == 0:
+                st_qa(s // 2)
+            else:
+                st_qs(s // 2)
+            if s == 2:
+                quant_w(gwb, wbq, wbs)
             if s + 3 >= 2:
                 st_f(s + 3)
-            if s + 5 >= 3:
+            if s == 3:
+                wc_c(3, False)
+                quant_w(gwc, wcq, wcs)
+            if s + 5 >= 4:
                 st_k(s + 5)
             if s == -1:
                 wb_t(0, "ms")
@@ -448,16 +459,12 @@ def tile_efficient_skan_batch_t_kernel(tc, x, base_weight, grid, scale_sp, coef,
             if s == 1:
                 wb_c(3, False)
                 wc_c(0, False)
-                quant_w(gwb, wbq, wbs)
                 wc_t(1, "mb")
                 wc_t(2, "ms")
             if s == 2:
                 wc_c(1, True)
                 wc_c(2, False)
                 wc_t(3, "ms")
-            if s == 3:
-                wc_c(3, False)
-                quant_w(gwc, wcq, wcs)
             if s >= 1 and s % 4 == 1 and s // 4 + 4 < TILES // GROUP:
                 load_x(s // 4 + 4)
 
@@ -466,8 +473,7 @@ def tile_efficient_skan_batch_t_kernel(tc, x, base_weight, grid, scale_sp, coef,
         st_ex(30)
         st_b(25)
         st_a(26)
-        st_qa(31)
-        st_qs(30)
+        st_qa(15)
         st_to(24)
         st_mxs(26)
         half_mxb(0, 0, "xt")
@@ -480,7 +486,7 @@ def tile_efficient_skan_batch_t_kernel(tc, x, base_weight, grid, scale_sp, coef,
         half_a(0, 1)
         st_ex(31)
         st_b(26)
-        st_qs(31)
+        st_qs(15)
         st_to(25)
         st_c(25)
         st_mxs(27)

@@ -36,7 +36,7 @@ def tile_efficient_skan_batch_t_kernel(tc, x, base_weight, grid, scale_sp, coef,
         kpool = ctx.enter_context(tc.tile_pool(name="kpool", bufs=2))
         fpool = ctx.enter_context(tc.tile_pool(name="fpool", bufs=4))
         gpool = ctx.enter_context(tc.tile_pool(name="gpool", bufs=3))
-        qpool = ctx.enter_context(tc.tile_pool(name="qpool", bufs=3))
+        qpool = ctx.enter_context(tc.tile_pool(name="qpool", bufs=5))
         tbpool = ctx.enter_context(tc.tile_pool(name="tbpool", bufs=5))
         otpool = ctx.enter_context(tc.tile_pool(name="otpool", bufs=6))
         ospool = ctx.enter_context(tc.tile_pool(name="ospool", bufs=8))
@@ -235,43 +235,26 @@ def tile_efficient_skan_batch_t_kernel(tc, x, base_weight, grid, scale_sp, coef,
                 func=ACT.Silu,
             )
 
-        def operand_of(pair):
-            if pair < HALF0 // 2:
-                return pair // 2, pair % 2, 2
-            return HALF0 // GROUP + pair - HALF0 // 2, 0, 1
-
-        def quant_pair(pair, grouped, codes, scales):
-            key, place, w = operand_of(pair)
-            for g in range(2):
-                cols = slice((g * w + place) * 256, (g * w + place + 1) * 256)
-                nc.vector.quantize_mx(
-                    out=codes[:, cols].bitcast(FP8X4), scales=scales[:, cols], in_=grouped[:, g * 1024 : (g + 1) * 1024]
-                )
-
         def st_qa(pair):
             if pair < 0 or pair >= TILES // 2:
                 return
-            key, place, w = operand_of(pair)
-            if place == 0:
-                aq[key] = qpool.tile([P, 1024], U32, name="aq", tag="aq", align_bytes=64)
-                asc[key] = qpool.tile([P, 1024], U8, name="asc", tag="asc", align_bytes=64)
-            quant_pair(pair, gat[pair], aq[key], asc[key])
+            aq[pair] = qpool.tile([P, 512], U32, name="aq", tag="aq", align_bytes=64)
+            asc[pair] = qpool.tile([P, 512], U8, name="asc", tag="asc", align_bytes=64)
+            nc.vector.quantize_mx(out=aq[pair][:].bitcast(FP8X4), scales=asc[pair][:], in_=gat[pair][:])
 
         def st_qs(pair):
             if pair < 0 or pair >= TILES // 2:
                 return
-            key, place, w = operand_of(pair)
-            if place == 0:
-                sq[key] = qpool.tile([P, 1024], U32, name="sq", tag="sq", align_bytes=64)
-                ssc[key] = qpool.tile([P, 1024], U8, name="ssc", tag="ssc", align_bytes=64)
-            quant_pair(pair, gst[pair], sq[key], ssc[key])
+            sq[pair] = qpool.tile([P, 512], U32, name="sq", tag="sq", align_bytes=64)
+            ssc[pair] = qpool.tile([P, 512], U8, name="ssc", tag="ssc", align_bytes=64)
+            nc.vector.quantize_mx(out=sq[pair][:].bitcast(FP8X4), scales=ssc[pair][:], in_=gst[pair][:])
 
-        def mx_group(acc, c, wq, ws, dq, dsc):
+        def mx_pair(acc, c, wq, ws, dq, dsc):
             for g in range(2):
                 wcols = slice(g * 512 + c * P, g * 512 + (c + 1) * P)
-                dcols = slice(g * 512, (g + 1) * 512)
+                dcols = slice(g * 256, (g + 1) * 256)
                 nc.tensor.matmul_mx(
-                    out=acc[:],
+                    out=acc,
                     lhsT=wq[:, wcols].bitcast(FP8X4),
                     lhsT_scale=ws[:, wcols],
                     rhs=dq[:, dcols].bitcast(FP8X4),
@@ -280,17 +263,22 @@ def tile_efficient_skan_batch_t_kernel(tc, x, base_weight, grid, scale_sp, coef,
                     stop=(g == 1),
                 )
 
+        def mx_group(acc, e, wq, ws, dq, dsc):
+            for h in range(2):
+                pair = 2 * (e // CHUNKS) + h
+                mx_pair(acc[:, h * 256 : (h + 1) * 256], e % CHUNKS, wq, ws, dq[pair], dsc[pair])
+
         def st_mxb(e, kind="mb"):
             if e < 0 or e >= HALF0:
                 return
             bps[e] = bank(kind, "bps")
-            mx_group(bps[e], e % CHUNKS, wbq, wbs, aq[e // CHUNKS], asc[e // CHUNKS])
+            mx_group(bps[e], e, wbq, wbs, aq, asc)
 
         def st_mxs(e, kind="ms"):
             if e < 0 or e >= HALF0:
                 return
             sps[e] = bank(kind, "sps")
-            mx_group(sps[e], e % CHUNKS, wcq, wcs, sq[e // CHUNKS], ssc[e // CHUNKS])
+            mx_group(sps[e], e, wcq, wcs, sq, ssc)
 
         def st_a(e):
             if e < 0 or e >= HALF0:
@@ -336,31 +324,17 @@ def tile_efficient_skan_batch_t_kernel(tc, x, base_weight, grid, scale_sp, coef,
         hot = {}
         hps = {}
 
-        def half_mx(h, pc, wq, ws, dq, dsc, kind):
-            acc = bank(kind, "hacc")
-            for ci in range(2):
-                c = 2 * pc + ci
-                for g in range(2):
-                    wcols = slice(g * 512 + c * P, g * 512 + (c + 1) * P)
-                    dcols = slice(g * 256, (g + 1) * 256)
-                    nc.tensor.matmul_mx(
-                        out=acc[:, ci * 256 : (ci + 1) * 256],
-                        lhsT=wq[:, wcols].bitcast(FP8X4),
-                        lhsT_scale=ws[:, wcols],
-                        rhs=dq[:, dcols].bitcast(FP8X4),
-                        rhs_scale=dsc[:, dcols],
-                        start=(g == 0),
-                        stop=(g == 1),
-                    )
-            return acc
-
         def half_mxb(h, pc, kind):
-            key = HALF0 // GROUP + h
-            hb[(h, pc)] = half_mx(h, pc, wbq, wbs, aq[key], asc[key], kind)
+            hb[(h, pc)] = bank(kind, "hacc")
+            pair = HALF0 // 2 + h
+            for ci in range(2):
+                mx_pair(hb[(h, pc)][:, ci * 256 : (ci + 1) * 256], 2 * pc + ci, wbq, wbs, aq[pair], asc[pair])
 
         def half_mxs(h, pc, kind):
-            key = HALF0 // GROUP + h
-            hs[(h, pc)] = half_mx(h, pc, wcq, wcs, sq[key], ssc[key], kind)
+            hs[(h, pc)] = bank(kind, "hacc")
+            pair = HALF0 // 2 + h
+            for ci in range(2):
+                mx_pair(hs[(h, pc)][:, ci * 256 : (ci + 1) * 256], 2 * pc + ci, wcq, wcs, sq[pair], ssc[pair])
 
         def half_a(h, pc):
             t = tbpool.tile([P, 512], F32, name="tb", tag="tb")
@@ -433,14 +407,14 @@ def tile_efficient_skan_batch_t_kernel(tc, x, base_weight, grid, scale_sp, coef,
             st_mxs(s - 4)
             st_ts(s + 1)
             st_sin(s + 2)
-            if s % 2 == 0:
-                st_qa(s // 2)
-            else:
-                st_qs(s // 2)
             if s == 2:
                 quant_w(gwb, wbq, wbs)
             if s + 3 >= 2:
                 st_f(s + 3)
+            if s % 2 == 0:
+                st_qa(s // 2)
+            else:
+                st_qs(s // 2)
             if s == 3:
                 wc_c(3, False)
                 quant_w(gwc, wcq, wcs)

@@ -70,18 +70,18 @@ def tile_efficient_skan_batch_t_kernel(tc, x, base_weight, grid, scale_sp, coef,
         ops = {}
         wps = {}
 
+        def load_part(grp, j, n):
+            if j == 0:
+                xt[grp] = xpool.tile([P, GROUP * KDIM], BF16, name="x_nat", tag="x_nat")
+            nc.sync.dma_start(
+                out=xt[grp][:, j * KDIM : (j + n) * KDIM],
+                in_=xf[grp * 512 : (grp + 1) * 512, :].rearrange("(p j) k -> p (j k)", j=GROUP)[
+                    :, j * KDIM : (j + n) * KDIM
+                ],
+            )
+
         def load_x(grp):
-            t = xpool.tile([P, GROUP * KDIM], BF16, name="x_nat", tag="x_nat")
-            rows = xf[grp * 512 : (grp + 1) * 512, :]
-            if grp == 0:
-                for j in range(GROUP):
-                    nc.sync.dma_start(
-                        out=t[:, j * KDIM : (j + 1) * KDIM],
-                        in_=rows.rearrange("(p j) k -> p j k", j=GROUP)[:, j, :],
-                    )
-            else:
-                nc.sync.dma_start(out=t[:], in_=rows.rearrange("(p j) k -> p (j k)", j=GROUP))
-            xt[grp] = t
+            load_part(grp, 0, GROUP)
 
         vecs = const.tile([P, P], BF16, name="vecs")
         nc.vector.memset(vecs[:], 0.0)
@@ -90,13 +90,15 @@ def tile_efficient_skan_batch_t_kernel(tc, x, base_weight, grid, scale_sp, coef,
         nc.scalar.dma_start(out=vecs[0:4, :], in_=scale_sp.rearrange("(a p) -> a p", p=P))
         nc.scalar.dma_start(out=vecs[4:8, :], in_=conv_b.rearrange("o (a p) -> (o a) p", p=P))
         nc.scalar.dma_start(out=vecs[8:16, :], in_=coef.rearrange("(a p) o -> a (p o)", p=P))
-        load_x(0)
+        for j in range(GROUP):
+            load_part(0, j, 1)
+        load_part(1, 0, 2)
         wb_nat = wstage.tile([P, CHUNKS * KDIM], BF16, name="wb_nat")
         nc.sync.dma_start(
             out=wb_nat[:].rearrange("p (c k) -> p c k", c=CHUNKS),
             in_=base_weight.rearrange("(c p) k -> p c k", p=P),
         )
-        load_x(1)
+        load_part(1, 2, 2)
         wc_nat = wstage.tile([P, CHUNKS * KDIM], BF16, name="wc_nat")
         nc.sync.dma_start(
             out=wc_nat[:].rearrange("p (c k) -> p c k", c=CHUNKS),
@@ -396,11 +398,13 @@ def tile_efficient_skan_batch_t_kernel(tc, x, base_weight, grid, scale_sp, coef,
         nc.vector.tensor_tensor(out=spb[:], in0=vps[:, 4:8], in1=vt[:, 0:4], op=ALU.mult)
 
         for s in range(-5, 30):
-            st_mxb(s - 4)
+            if s < 29:
+                st_mxb(s - 4)
             st_ex(s)
             st_b(s - 5)
             st_silu(s + 2)
-            st_a(s - 4)
+            if s < 29:
+                st_a(s - 4)
             st_to(s - 6)
             st_c(s - 6)
             st_tx(s + 3)
@@ -432,7 +436,7 @@ def tile_efficient_skan_batch_t_kernel(tc, x, base_weight, grid, scale_sp, coef,
                 wc_t(0, "ms")
             if s == 1:
                 wb_c(3, False)
-                wc_c(0, False)
+                wc_c(0, True)
                 wc_t(1, "mb")
                 wc_t(2, "ms")
             if s == 2:
@@ -441,34 +445,37 @@ def tile_efficient_skan_batch_t_kernel(tc, x, base_weight, grid, scale_sp, coef,
                 wc_t(3, "ms")
             if s >= 1 and s % 4 == 1 and s // 4 + 4 < TILES // GROUP:
                 load_x(s // 4 + 4)
+            if s == 28:
+                st_mxb(25, "xt")
+                st_mxb(26)
+            if s == 29:
+                st_a(25)
+                st_a(26)
+                st_mxb(27, "xt")
+                st_a(27)
 
-
-        st_mxb(26)
         st_ex(30)
         st_b(25)
-        st_a(26)
-        st_qa(15)
-        st_to(24)
         st_mxs(26)
-        half_mxb(0, 0, "xt")
-        half_a(0, 0)
+        st_to(24)
         st_c(24)
+        half_mxb(0, 0, "mb")
+        half_a(0, 0)
         st_ts(31)
-        st_mxb(27)
         half_mxb(0, 1, "xt")
-        st_a(27)
         half_a(0, 1)
+        st_qa(15)
         st_ex(31)
         st_b(26)
         st_qs(15)
+        st_mxs(27)
         st_to(25)
         st_c(25)
-        st_mxs(27)
         half_mxs(0, 0, "ms")
         half_mxs(0, 1, "mb")
         half_mxb(1, 0, "xt")
-        half_mxb(1, 1, "xt")
         half_a(1, 0)
+        half_mxb(1, 1, "xt")
         half_a(1, 1)
         st_to(26)
         st_c(26)

import math
from contextlib import ExitStack

import concourse.masks as masks
import concourse.mybir as mybir

FLOPS = 2 * 2 * 4096 * 1024 * 512

P = 128
F32 = mybir.dt.float32
BF16 = mybir.dt.bfloat16
I32 = mybir.dt.int32
U32 = mybir.dt.uint32
U8 = mybir.dt.uint8
FP8X4 = mybir.dt.float8_e4m3fn_x4
ALU = mybir.AluOpType
ACT = mybir.ActivationFunctionType

TILES = 32
HALF0 = 28
GROUP = 4
CHUNKS = 4
KDIM = 1024
NOUT = 512
TWO_PI = 2.0 * math.pi


def tile_efficient_skan_batch_t_kernel(tc, x, base_weight, grid, scale_sp, coef, conv_w, conv_b, out):
    nc = tc.nc
    xf = x.flatten_outer_dims()
    of = out.flatten_outer_dims()
    with ExitStack() as ctx:
        const = ctx.enter_context(tc.tile_pool(name="const", bufs=1))
        wstage = ctx.enter_context(tc.tile_pool(name="wstage", bufs=1))
        xpool = ctx.enter_context(tc.tile_pool(name="xpool", bufs=4))
        kpool = ctx.enter_context(tc.tile_pool(name="kpool", bufs=2))
        fpool = ctx.enter_context(tc.tile_pool(name="fpool", bufs=4))
        gpool = ctx.enter_context(tc.tile_pool(name="gpool", bufs=3))
        qpool = ctx.enter_context(tc.tile_pool(name="qpool", bufs=5))
        tbpool = ctx.enter_context(tc.tile_pool(name="tbpool", bufs=5))
        otpool = ctx.enter_context(tc.tile_pool(name="otpool", bufs=6))
        ospool = ctx.enter_context(tc.tile_pool(name="ospool", bufs=8))
        ps_xt = ctx.enter_context(tc.psum_pool(name="ps_xt", bufs=2))
        ps_sn = ctx.enter_context(tc.psum_pool(name="ps_sn", bufs=2))
        ps_mb = ctx.enter_context(tc.psum_pool(name="ps_mb", bufs=1))
        ps_ms = ctx.enter_context(tc.psum_pool(name="ps_ms", bufs=2))
        ps_op = ctx.enter_context(tc.psum_pool(name="ps_op", bufs=1))
        ctx.enter_context(tc.manual_schedule())

        psum = {"xt": ps_xt, "sn": ps_sn, "mb": ps_mb, "ms": ps_ms, "op": ps_op}

        def bank(kind, name, dtype=F32, cols=512):
            return psum[kind].tile([P, cols], dtype, name=name, tag=kind)

        xt = {}
        kt = {}
        ft = {}
        xps = {}
        snps = {}
        gat = {}
        gst = {}
        aq = {}
        asc = {}
        sq = {}
        ssc = {}
        bps = {}
        sps = {}
        tbt = {}
        ott = {}
        ops = {}
        wps = {}

        def load_part(grp, j, n):
            if j == 0:
                xt[grp] = xpool.tile([P, GROUP * KDIM], BF16, name="x_nat", tag="x_nat")
            nc.sync.dma_start(
                out=xt[grp][:, j * KDIM : (j + n) * KDIM],
                in_=xf[grp * 512 : (grp + 1) * 512, :].rearrange("(p j) k -> p (j k)", j=GROUP)[
                    :, j * KDIM : (j + n) * KDIM
                ],
            )

        def load_x(grp):
            load_part(grp, 0, GROUP)

        vecs = const.tile([P, P], BF16, name="vecs")
        nc.vector.memset(vecs[:], 0.0)
        g_bf = const.tile([P, 1], BF16, name="g_bf")
        nc.scalar.dma_start(out=g_bf[:], in_=grid.partition_broadcast(P))
        nc.scalar.dma_start(out=vecs[0:4, :], in_=scale_sp.rearrange("(a p) -> a p", p=P))
        nc.scalar.dma_start(out=vecs[4:8, :], in_=conv_b.rearrange("o (a p) -> (o a) p", p=P))
        nc.scalar.dma_start(out=vecs[8:16, :], in_=coef.rearrange("(a p) o -> a (p o)", p=P))
        for j in range(GROUP):
            load_part(0, j, 1)
        load_part(1, 0, 2)
        wb_nat = wstage.tile([P, CHUNKS * KDIM], BF16, name="wb_nat")
        nc.sync.dma_start(
            out=wb_nat[:].rearrange("p (c k) -> p c k", c=CHUNKS),
            in_=base_weight.rearrange("(c p) k -> p c k", p=P),
        )
        load_part(1, 2, 2)
        wc_nat = wstage.tile([P, CHUNKS * KDIM], BF16, name="wc_nat")
        nc.sync.dma_start(
            out=wc_nat[:].rearrange("p (c k) -> p c k", c=CHUNKS),
            in_=conv_w.rearrange("o (c p) k -> p (o c) k", p=P),
        )
        load_x(2)
        load_x(3)

        ident_f = const.tile([P, P], F32, name="ident_f")
        masks.make_identity(nc, ident_f[:])
        ident_b = const.tile([P, P], BF16, name="ident_b")
        masks.make_identity(nc, ident_b[:])

        cyc = const.tile([P, 1], F32, name="cyc")
        nc.vector.tensor_scalar(out=cyc[:], in0=g_bf[:], scalar1=1.0 / TWO_PI, scalar2=None, op0=ALU.mult)

        gwb = wstage.tile([P, 4096], BF16, name="gwb", align_bytes=64)
        gwc = wstage.tile([P, 4096], BF16, name="gwc", align_bytes=64)
        wbq = const.tile([P, 1024], U32, name="wbq", align_bytes=64)
        wbs = const.tile([P, 1024], U8, name="wbs", align_bytes=64)
        wcq = const.tile([P, 1024], U32, name="wcq", align_bytes=64)
        wcs = const.tile([P, 1024], U8, name="wcs", align_bytes=64)

        def copy_out(on_vector, dst, srcv):
            if on_vector:
                nc.vector.tensor_copy(out=dst, in_=srcv)
            else:
                nc.scalar.copy(out=dst, in_=srcv)

        def wb_t(c, kind):
            ps = bank(kind, "wbps")
            words = wb_nat[:].bitcast(F32)
            for q in range(4):
                nc.tensor.transpose(
                    ps[:, q * P : (q + 1) * P], words[:, c * 512 + q * P : c * 512 + (q + 1) * P], ident_f[:]
                )
            wps[("b", c)] = ps

        def wb_c(c, on_vector):
            copy_out(
                on_vector,
                gwb[:].bitcast(F32).rearrange("p (g c m u) -> p g c m u", g=2, c=CHUNKS, u=2)[:, :, c, :, :],
                wps[("b", c)][:].rearrange("p (g u m) -> p g m u", g=2, u=2),
            )

        def wc_t(c, kind):
            ps = bank(kind, "wcps", BF16, 1024)
            for b in range(8):
                nc.tensor.transpose(
                    ps[:, b * P : (b + 1) * P], wc_nat[:, c * KDIM + b * P : c * KDIM + (b + 1) * P], ident_b[:]
                )
            wps[("c", c)] = ps

        def wc_c(c, on_vector):
            copy_out(
                on_vector,
                gwc[:].rearrange("p (g c m t) -> p g c m t", g=2, c=CHUNKS, t=4)[:, :, c, :, :],
                wps[("c", c)][:].rearrange("p (g t m) -> p g m t", g=2, t=4),
            )

        def quant_w(grouped, codes, scales):
            nc.vector.quantize_mx(out=codes[:].bitcast(FP8X4), scales=scales[:], in_=grouped[:])

        def x_of(tau):
            return xt[tau // GROUP][:, (tau % GROUP) * KDIM : (tau % GROUP + 1) * KDIM]

        def st_k(tau, on_vector=False):
            if tau < 0 or tau >= TILES:
                return
            t = kpool.tile([P, KDIM], I32, name="kint", tag="kint")
            eng = nc.vector if on_vector else nc.gpsimd
            eng.tensor_scalar(out=t[:], in0=x_of(tau), scalar1=cyc[:, 0:1], scalar2=0.0, op0=ALU.mult, op1=ALU.add)
            kt[tau] = t

        def st_f(tau):
            if tau < 0 or tau >= TILES:
                return
            t = fpool.tile([P, KDIM], F32, name="frac", tag="frac")
            nc.vector.scalar_tensor_tensor(
                out=t[:], in0=x_of(tau), scalar=cyc[:, 0:1], in1=kt[tau][:], op0=ALU.mult, op1=ALU.subtract
            )
            ft[tau] = t

        def st_sin(tau):
            if tau < 0 or tau >= TILES:
                return
            nc.scalar.activation(out=ft[tau][:], in_=ft[tau][:], func=ACT.Sin, scale=TWO_PI)

        def st_ts(tau):
            if tau < 0 or tau >= TILES:
                return
            for g in range(2):
                ps = bank("sn", "snps")
                for t in range(4):
                    b = 4 * g + t
                    nc.tensor.transpose(ps[:, t * P : (t + 1) * P], ft[tau][:, b * P : (b + 1) * P], ident_f[:])
                snps[(tau, g)] = ps

        def st_ex(tau):
            if tau < 0 or tau >= TILES:
                return
            i = tau % 2
            if i == 0:
                gst[tau // 2] = gpool.tile([P, 2048], BF16, name="gs", tag="gs", align_bytes=64)
            t = gst[tau // 2]
            for g in range(2):
                nc.vector.tensor_tensor(
                    out=t[:, g * 1024 + i * 512 : g * 1024 + (i + 1) * 512].rearrange("p (r t) -> p r t", t=4),
                    in0=snps[(tau, g)][:].rearrange("p (t r) -> p r t", t=4),
                    in1=vt[:, 8 + 4 * g : 12 + 4 * g].unsqueeze(1).to_broadcast([P, P, 4]),
                    op=ALU.mult,
                )

        def st_tx(tau):
            if tau < 0 or tau >= TILES:
                return
            ps = bank("xt", "xps")
            words = xt[tau // GROUP][:].bitcast(F32)
            base = (tau % GROUP) * 512
            for q in range(4):
                place = 2 * (q % 2) + q // 2
                nc.tensor.transpose(
                    ps[:, place * P : (place + 1) * P], words[:, base + q * P : base + (q + 1) * P], ident_f[:]
                )
            xps[tau] = ps

        def st_silu(tau):
            if tau < 0 or tau >= TILES:
                return
            i = tau % 2
            if i == 0:
                gat[tau // 2] = gpool.tile([P, 2048], BF16, name="ga", tag="ga", align_bytes=64)
            nc.scalar.activation(
                out=gat[tau // 2][:].rearrange("p (g i r u e) -> p g i r u e", g=2, i=2, u=2, e=2)[:, :, i],
                in_=xps[tau][:].bitcast(BF16).rearrange("p (u g r e) -> p g r u e", u=2, g=2, e=2),
                func=ACT.Silu,
            )

        def st_qa(pair):
            if pair < 0 or pair >= TILES // 2:
                return
            aq[pair] = qpool.tile([P, 512], U32, name="aq", tag="aq", align_bytes=64)
            asc[pair] = qpool.tile([P, 512], U8, name="asc", tag="asc", align_bytes=64)
            nc.vector.quantize_mx(out=aq[pair][:].bitcast(FP8X4), scales=asc[pair][:], in_=gat[pair][:])

        def st_qs(pair):
            if pair < 0 or pair >= TILES // 2:
                return
            sq[pair] = qpool.tile([P, 512], U32, name="sq", tag="sq", align_bytes=64)
            ssc[pair] = qpool.tile([P, 512], U8, name="ssc", tag="ssc", align_bytes=64)
            nc.vector.quantize_mx(out=sq[pair][:].bitcast(FP8X4), scales=ssc[pair][:], in_=gst[pair][:])

        def mx_pair(acc, c, wq, ws, dq, dsc):
            for g in range(2):
                wcols = slice(g * 512 + c * P, g * 512 + (c + 1) * P)
                dcols = slice(g * 256, (g + 1) * 256)
                nc.tensor.matmul_mx(
                    out=acc,
                    lhsT=wq[:, wcols].bitcast(FP8X4),
                    lhsT_scale=ws[:, wcols],
                    rhs=dq[:, dcols].bitcast(FP8X4),
                    rhs_scale=dsc[:, dcols],
                    start=(g == 0),
                    stop=(g == 1),
                )

        def mx_group(acc, e, wq, ws, dq, dsc):
            for h in range(2):
                pair = 2 * (e // CHUNKS) + h
                mx_pair(acc[:, h * 256 : (h + 1) * 256], e % CHUNKS, wq, ws, dq[pair], dsc[pair])

        def st_mxb(e, kind="mb"):
            if e < 0 or e >= HALF0:
                return
            bps[e] = bank(kind, "bps")
            mx_group(bps[e], e, wbq, wbs, aq, asc)

        def st_mxs(e, kind="ms"):
            if e < 0 or e >= HALF0:
                return
            sps[e] = bank(kind, "sps")
            mx_group(sps[e], e, wcq, wcs, sq, ssc)

        def st_a(e):
            if e < 0 or e >= HALF0:
                return
            c = e % CHUNKS
            t = tbpool.tile([P, 512], F32, name="tb", tag="tb")
            nc.scalar.activation(out=t[:], in_=bps[e][:], func=ACT.Identity, bias=spb[:, c : c + 1], scale=1.0)
            tbt[e] = t

        def st_b(e):
            if e < 0 or e >= HALF0:
                return
            c = e % CHUNKS
            t = otpool.tile([P, 512], F32, name="ot", tag="ot")
            nc.vector.scalar_tensor_tensor(
                out=t[:], in0=sps[e][:], scalar=vt[:, c : c + 1], in1=tbt[e][:], op0=ALU.mult, op1=ALU.add
            )
            ott[e] = t

        def st_to(e, kind="op"):
            if e < 0 or e >= HALF0:
                return
            ps = bank(kind, "ops")
            for j in range(GROUP):
                nc.tensor.transpose(ps[:, j * P : (j + 1) * P], ott[e][:, j * P : (j + 1) * P], ident_f[:])
            ops[e] = ps

        def st_c(e, on_vector=False):
            if e < 0 or e >= HALF0:
                return
            grp = e // CHUNKS
            c = e % CHUNKS
            t = ospool.tile([P, 512], F32, name="osb", tag="osb")
            copy_out(on_vector, t[:], ops[e][:])
            nc.sync.dma_start(
                out=of[grp * 512 : (grp + 1) * 512, :].rearrange("(p j) f -> p j f", j=GROUP)[:, :, c * P : (c + 1) * P],
                in_=t[:].rearrange("p (j f) -> p j f", j=GROUP),
            )

        hb = {}
        hs = {}
        htb = {}
        hot = {}
        hps = {}

        def half_mxb(h, pc, kind):
            hb[(h, pc)] = bank(kind, "hacc")
            pair = HALF0 // 2 + h
            for ci in range(2):
                mx_pair(hb[(h, pc)][:, ci * 256 : (ci + 1) * 256], 2 * pc + ci, wbq, wbs, aq[pair], asc[pair])

        def half_mxs(h, pc, kind):
            hs[(h, pc)] = bank(kind, "hacc")
            pair = HALF0 // 2 + h
            for ci in range(2):
                mx_pair(hs[(h, pc)][:, ci * 256 : (ci + 1) * 256], 2 * pc + ci, wcq, wcs, sq[pair], ssc[pair])

        def half_a(h, pc):
            t = tbpool.tile([P, 512], F32, name="tb", tag="tb")
            for ci in range(2):
                c = 2 * pc + ci
                cols = slice(ci * 256, (ci + 1) * 256)
                nc.scalar.activation(
                    out=t[:, cols], in_=hb[(h, pc)][:, cols], func=ACT.Identity, bias=spb[:, c : c + 1], scale=1.0
                )
            htb[(h, pc)] = t

        def half_b(h, pc):
            t = otpool.tile([P, 512], F32, name="ot", tag="ot")
            for ci in range(2):
                c = 2 * pc + ci
                cols = slice(ci * 256, (ci + 1) * 256)
                nc.vector.scalar_tensor_tensor(
                    out=t[:, cols],
                    in0=hs[(h, pc)][:, cols],
                    scalar=vt[:, c : c + 1],
                    in1=htb[(h, pc)][:, cols],
                    op0=ALU.mult,
                    op1=ALU.add,
                )
            hot[(h, pc)] = t

        def half_to(h, pc, kind):
            ps = bank(kind, "hps")
            for ci in range(2):
                for j in range(2):
                    nc.tensor.transpose(
                        ps[:, j * 256 + ci * P : j * 256 + (ci + 1) * P],
                        hot[(h, pc)][:, ci * 256 + j * P : ci * 256 + (j + 1) * P],
                        ident_f[:],
                    )
            hps[(h, pc)] = ps

        def half_c(h, pc, on_vector=False):
            t = ospool.tile([P, 512], F32, name="osb", tag="osb")
            copy_out(on_vector, t[:], hps[(h, pc)][:])
            nc.sync.dma_start(
                out=of[HALF0 * P : TILES * P, :].rearrange("(p j) f -> p j f", j=GROUP)[
                    :, 2 * h : 2 * h + 2, pc * 256 : (pc + 1) * 256
                ],
                in_=t[:].rearrange("p (j f) -> p j f", j=2),
            )

        st_k(0, True)
        st_k(1, True)
        st_f(0)
        st_f(1)
        st_k(2, True)
        st_k(3, True)
        vps = bank("op", "vps", BF16, P)
        nc.tensor.transpose(vps[:], vecs[:], ident_b[:])
        vt = const.tile([P, 16], F32, name="vt")
        nc.vector.tensor_copy(out=vt[:], in_=vps[:, 0:16])
        spb = const.tile([P, CHUNKS], F32, name="spb")
        nc.vector.tensor_tensor(out=spb[:], in0=vps[:, 4:8], in1=vt[:, 0:4], op=ALU.mult)

        for s in range(-5, 30):
            if s < 29:
                st_mxb(s - 4)
            st_ex(s)
            st_b(s - 5)
            st_silu(s + 2)
            if s < 29:
                st_a(s - 4)
            st_to(s - 6)
            st_c(s - 6)
            st_tx(s + 3)
            st_mxs(s - 4)
            st_ts(s + 1)
            st_sin(s + 2)
            if s == 2:
                quant_w(gwb, wbq, wbs)
            if s + 3 >= 2:
                st_f(s + 3)
            if s % 2 == 0:
                st_qa(s // 2)
            else:
                st_qs(s // 2)
            if s == 3:
                wc_c(3, False)
                quant_w(gwc, wcq, wcs)
            if s + 5 >= 4:
                st_k(s + 5)
            if s == -1:
                wb_t(0, "ms")
                wb_t(1, "ms")
                wb_t(2, "mb")
            if s == 0:
                wb_c(0, False)
                wb_c(1, False)
                wb_c(2, False)
                wb_t(3, "ms")
                wc_t(0, "ms")
            if s == 1:
                wb_c(3, False)
                wc_c(0, True)
                wc_t(1, "mb")
                wc_t(2, "ms")
            if s == 2:
                wc_c(1, True)
                wc_c(2, False)
                wc_t(3, "ms")
            if s >= 1 and s % 4 == 1 and s // 4 + 4 < TILES // GROUP:
                load_x(s // 4 + 4)
            if s == 28:
                st_mxb(25, "xt")
                st_mxb(26)
            if s == 29:
                st_a(25)
                st_a(26)
                st_mxb(27, "xt")
                st_a(27)

        st_ex(30)
        st_b(25)
        st_mxs(26)
        st_to(24)
        st_c(24)
        half_mxb(0, 0, "mb")
        half_a(0, 0)
        st_ts(31)
        half_mxb(0, 1, "xt")
        half_a(0, 1)
        st_qa(15)
        st_ex(31)
        st_b(26)
        st_qs(15)
        st_mxs(27)
        st_to(25)
        st_c(25)
        half_mxs(0, 0, "ms")
        half_mxs(0, 1, "mb")
        half_mxb(1, 0, "xt")
        half_a(1, 0)
        half_mxb(1, 1, "xt")
        half_a(1, 1)
        st_to(26)
        st_c(26)
        half_mxs(1, 0, "sn")
        half_mxs(1, 1, "sn")
        st_b(27)
        half_b(0, 0)
        half_b(0, 1)
        half_b(1, 0)
        half_b(1, 1)
        st_to(27, "ms")
        st_c(27)
        half_to(0, 0, "op")
        half_c(0, 0)
        half_to(0, 1, "xt")
        half_c(0, 1, True)
        half_to(1, 0, "xt")
        half_c(1, 0)
        half_to(1, 1, "mb")
        half_c(1, 1, True)
